import numpy as np
import ml_dtypes


def mxq(x, axis, fmt="e4m3"):
    dtype, down = {"e4m3": (ml_dtypes.float8_e4m3fn, 7), "e5m2": (ml_dtypes.float8_e5m2, 14)}[fmt]
    v = np.moveaxis(np.asarray(x, np.float32).astype(ml_dtypes.bfloat16).astype(np.float64), axis, -1)
    blocks = v.reshape(v.shape[:-1] + (-1, 32))
    amax = np.abs(blocks).max(-1, keepdims=True)
    byte = np.maximum(np.where(amax > 0, np.frexp(amax)[1] - 1 + 127, 0) - down, 1)
    scale = np.exp2(byte - 127.0)
    codes = (blocks / scale).astype(np.float32).astype(dtype).astype(np.float64)
    return np.moveaxis((codes * scale).reshape(v.shape), -1, axis)


WIDE = False


def mx_kscale(k):
    if not WIDE:
        return np.ones(k)
    levels = np.array([10, -10, 5, -5, 0])
    a = np.random.permutation(np.resize(levels, k // 512 * 4)).reshape(k // 512, 4)
    idx = np.arange(k)
    return np.exp2(a[idx // 512, idx % 128 // 32])


BF16 = ml_dtypes.bfloat16


def bf(x):
    return np.asarray(x, np.float32).astype(BF16)


def f64(x):
    return np.asarray(x).astype(np.float64)


B, S, D, H, C = 4, 2048, 256, 512, 512
F = 2 * D
LN_EPS = 1e-5


def erf(u):
    a = np.clip(u, -6.0, 6.0)
    w = 2.0 * a * a
    term = a.copy()
    tot = a.copy()
    for n in range(1, 100):
        term = term * w / (2 * n + 1)
        tot = tot + term
    return 2.0 / np.sqrt(np.pi) * np.exp(-a * a) * tot


def gelu_erf(z):
    return 0.5 * z * (1.0 + erf(z / np.sqrt(2.0)))


def setup_inputs():
    s = mx_kscale(H)
    return {"h_ret": bf(np.random.standard_normal((B, S, H)) * 3.0 * s),
            "x": bf(np.random.standard_normal((B, S, D))),
            "W1": bf(np.random.standard_normal((F, H)) * 0.3 / np.sqrt(H) / s),
            "b1": bf(np.random.standard_normal(F) * 0.2),
            "W2": bf(np.random.standard_normal((D, F)) * 1.5 / np.sqrt(F)),
            "b2": bf(np.random.standard_normal(D) * 0.2),
            "ln_g": bf(1.0 + 0.1 * np.random.standard_normal(D)),
            "ln_b": bf(0.1 * np.random.standard_normal(D))}


def reference(h_ret, x, W1, b1, W2, b2, ln_g, ln_b):
    z = (mxq(f64(h_ret), 2, "e4m3") @ mxq(f64(W1), 1, "e4m3").T) + f64(b1)
    g = gelu_erf(z)
    o = (mxq(g, 2, "e4m3") @ mxq(f64(W2), 1, "e4m3").T) + f64(b2)
    y = f64(x) + o
    mu = y.mean(-1, keepdims=True)
    var = np.square(y - mu).mean(-1, keepdims=True)
    return (y - mu) / np.sqrt(var + LN_EPS) * f64(ln_g) + f64(ln_b)

@@ -1,0 +1,288 @@
+from contextlib import ExitStack
+
+import concourse.mybir as mybir
+from concourse.masks import make_identity
+
+F32 = mybir.dt.float32
+BF16 = mybir.dt.bfloat16
+U32 = mybir.dt.uint32
+U8 = mybir.dt.uint8
+FP8X4 = mybir.dt.float8_e4m3fn_x4
+ALU = mybir.AluOpType
+ACT = mybir.ActivationFunctionType
+
+P = 128
+TOKENS = 4 * 2048
+H = 512
+F = 512
+D = 256
+GROUP = 512
+TILES = GROUP // P
+N_GROUPS = TOKENS // GROUP
+LN_EPS = 1e-5
+SCALAR_TILES = 0
+
+FLOPS = 2 * TOKENS * H * F + 2 * TOKENS * F * D
+
+
+def tile_simplifiedretnet_pb_t_kernel(tc, h_ret, x, W1, b1, W2, b2, ln_g, ln_b, out):
+    nc = tc.nc
+    h_view = h_ret.flatten_outer_dims().rearrange("(g p j) k -> g p j k", p=P, j=TILES)
+    x_view = x.flatten_outer_dims().rearrange("(g p j) d -> g p j d", p=P, j=TILES)
+    out_view = out.flatten_outer_dims().rearrange("(g p j) d -> g p j d", p=P, j=TILES)
+
+    with ExitStack() as ctx:
+        keep = ctx.enter_context(tc.tile_pool(name="keep", bufs=1))
+        two = ctx.enter_context(tc.tile_pool(name="two", bufs=2))
+        three = ctx.enter_context(tc.tile_pool(name="three", bufs=3))
+        four = ctx.enter_context(tc.tile_pool(name="four", bufs=4))
+        psum_t = ctx.enter_context(tc.psum_pool(name="psum_t", bufs=2))
+        psum_z = ctx.enter_context(tc.psum_pool(name="psum_z", bufs=3))
+        psum_o = ctx.enter_context(tc.psum_pool(name="psum_o", bufs=2))
+        psum_c = ctx.enter_context(tc.psum_pool(name="psum_c", bufs=1))
+        ctx.enter_context(tc.manual_schedule())
+
+        ident = keep.tile([P, P], F32, name="ident")
+        make_identity(nc, ident[:])
+        rows = keep.tile([P, 3 * D], BF16, name="rows")
+        nc.vector.memset(rows[:], 0.0)
+        ones = keep.tile([P, P], BF16, name="ones")
+        nc.vector.memset(ones[:], 1.0)
+        sixteens = keep.tile([P, P], BF16, name="sixteens")
+        nc.vector.memset(sixteens[:], 16.0)
+        minus_half = keep.tile([P, TILES], F32, name="minus_half")
+        nc.vector.memset(minus_half[:], -0.5)
+        b1_c = keep.tile([P, TILES], BF16, name="b1_c")
+        nc.scalar.dma_start(out=b1_c[:], in_=b1.rearrange("(m c) -> m c", c=TILES))
+        nc.scalar.dma_start(out=rows[0:1, 0:D], in_=b2.rearrange("(o d) -> o d", o=1))
+        nc.scalar.dma_start(out=rows[0:1, D:2 * D], in_=ln_g.rearrange("(o d) -> o d", o=1))
+        nc.scalar.dma_start(out=rows[0:1, 2 * D:3 * D], in_=ln_b.rearrange("(o d) -> o d", o=1))
+
+        w1_sb = keep.tile([P, TILES, H], BF16, name="w1_sb")
+        w2_sb = keep.tile([P, 2, F], BF16, name="w2_sb")
+        src = {"w": w1_sb}
+        x_sb = {}
+        for g in range(N_GROUPS):
+            src[g] = keep.tile([P, TILES, H], BF16, name="h%d" % g)
+            x_sb[g] = keep.tile([P, TILES, D], BF16, name="x%d" % g)
+        nc.sync.dma_start(out=w1_sb[:], in_=W1.rearrange("(m c) k -> m c k", c=TILES))
+        nc.sync.dma_start(out=src[0][:], in_=h_view[0])
+        nc.sync.dma_start(out=src[1][:], in_=h_view[1])
+        nc.sync.dma_start(out=w2_sb[:], in_=W2.rearrange("(a p) f -> p a f", p=P))
+        nc.sync.dma_start(out=src[2][:], in_=h_view[2])
+        nc.sync.dma_start(out=x_sb[0][:], in_=x_view[0])
+        nc.sync.dma_start(out=src[3][:], in_=h_view[3])
+        for g in range(1, N_GROUPS):
+            if g + 3 < N_GROUPS:
+                nc.sync.dma_start(out=src[g + 3][:], in_=h_view[g + 3])
+            nc.sync.dma_start(out=x_sb[g][:], in_=x_view[g])
+
+        w1_codes = keep.tile([P, F], U32, name="w1_codes", align_bytes=64)
+        w1_scales = keep.tile([P, F], U8, name="w1_scales", align_bytes=64)
+        w2_codes = keep.tile([P, D], U32, name="w2_codes", align_bytes=64)
+        w2_scales = keep.tile([P, D], U8, name="w2_scales", align_bytes=64)
+        ln_c = psum_c.tile([P, 2 * D], F32, name="ln_c")
+        b2_b = keep.tile([P, D], F32, name="b2_b")
+        lnb_b = keep.tile([P, D], F32, name="lnb_b")
+
+        banks = {}
+        grouped = {}
+        codes = {"w": (w1_codes, w1_scales)}
+        planes = {}
+        g_grouped = {}
+        g_codes = {}
+        o_banks = {}
+        xb = {}
+        y = {}
+        res = {}
+        stats = {}
+
+        def copy_out(engine, dst, source):
+            if engine == "vector":
+                nc.vector.tensor_copy(out=dst, in_=source)
+            else:
+                nc.scalar.copy(out=dst, in_=source)
+
+        def transposes(key):
+            words = src[key][:].bitcast(F32)
+            for b in range(2):
+                tp = psum_t.tile([P, 2, 2 * P], F32, name="tp")
+                for jj in range(2):
+                    for u in range(2):
+                        nc.tensor.transpose(
+                            tp[:, u, jj * P:(jj + 1) * P],
+                            words[:, 2 * b + jj, u * P:(u + 1) * P],
+                            ident[:],
+                        )
+                banks[(key, b)] = tp
+
+        def copies(key, engines=("scalar", "scalar")):
+            t = two.tile([P, 4 * GROUP], BF16, name="grouped", align_bytes=64)
+            grouped[key] = t
+            words = t[:].bitcast(F32).rearrange("p (t u) -> p t u", u=2)
+            for b in range(2):
+                copy_out(engines[b], words[:, b * 2 * P:(b + 1) * 2 * P, :],
+                         banks[(key, b)][:].rearrange("p u t -> p t u"))
+
+        def quantise(key):
+            if key != "w":
+                codes[key] = (three.tile([P, GROUP], U32, name="h_codes", align_bytes=64),
+                              three.tile([P, GROUP], U8, name="h_scales", align_bytes=64))
+            nc.vector.quantize_mx(out=codes[key][0][:].bitcast(FP8X4), scales=codes[key][1][:],
+                                  in_=grouped[key][:])
+
+        def second_weight():
+            words = w2_sb[:].bitcast(F32).rearrange("p a (q u) -> p a q u", u=2)
+            tp = psum_t.tile([P, 2, 2 * P], F32, name="tp")
+            for a in range(2):
+                for u in range(2):
+                    nc.tensor.transpose(tp[:, u, a * P:(a + 1) * P], words[:, a, :, u], ident[:])
+            t = keep.tile([P, 4 * D], BF16, name="w2_grouped", align_bytes=64)
+            nc.vector.tensor_copy(out=t[:].bitcast(F32).rearrange("p (d u) -> p d u", u=2),
+                                  in_=tp[:].rearrange("p u d -> p d u"))
+            nc.vector.quantize_mx(out=w2_codes[:].bitcast(FP8X4), scales=w2_scales[:], in_=t[:])
+
+        def constants():
+            nc.tensor.matmul(out=ln_c[:, 0:D], lhsT=sixteens[:], rhs=rows[:, D:2 * D],
+                             start=True, stop=True)
+            nc.tensor.matmul(out=ln_c[:, D:2 * D], lhsT=ones[:], rhs=rows[:, 2 * D:3 * D],
+                             start=True, stop=True)
+            o = psum_o.tile([P, 2, D], F32, name="o")
+            nc.tensor.matmul(out=o[:, 0, :], lhsT=ones[:], rhs=rows[:, 0:D], start=True, stop=True)
+            nc.vector.tensor_copy(out=b2_b[:], in_=o[:, 0, :])
+            if SCALAR_TILES:
+                nc.vector.tensor_copy(out=lnb_b[:], in_=ln_c[:, D:2 * D])
+
+        def first_matmul(g):
+            planes[g] = two.tile([P, TILES, GROUP], BF16, name="planes")
+            for c in range(TILES):
+                z = psum_z.tile([P, GROUP], F32, name="z")
+                nc.tensor.matmul_mx(
+                    out=z[:],
+                    lhsT=w1_codes[:, c * P:(c + 1) * P].bitcast(FP8X4),
+                    lhsT_scale=w1_scales[:, c * P:(c + 1) * P],
+                    rhs=codes[g][0][:].bitcast(FP8X4),
+                    rhs_scale=codes[g][1][:],
+                    start=True, stop=True,
+                )
+                nc.scalar.activation(out=planes[g][:, c, :], in_=z[:], func=ACT.Gelu,
+                                     bias=b1_c[:, c:c + 1], scale=1.0)
+
+        def regroup(g):
+            g_grouped[g] = two.tile([P, GROUP, 4], BF16, name="g_grouped", align_bytes=64)
+            nc.vector.tensor_copy(
+                out=g_grouped[g][:].rearrange("p (c i) t -> p c t i", i=4),
+                in_=planes[g][:].rearrange("p t (c i) -> p c t i", i=4),
+            )
+
+        def quantise_g(g):
+            g_codes[g] = (two.tile([P, GROUP], U32, name="g_codes", align_bytes=64),
+                          two.tile([P, GROUP], U8, name="g_scales", align_bytes=64))
+            nc.vector.quantize_mx(out=g_codes[g][0][:].bitcast(FP8X4), scales=g_codes[g][1][:],
+                                  in_=g_grouped[g][:].rearrange("p w j -> p (w j)"))
+
+        def add_bias(g):
+            xb[g] = four.tile([P, TILES, D], F32, name="xb")
+            nc.gpsimd.tensor_tensor(
+                out=xb[g][:], in0=x_sb[g][:],
+                in1=b2_b[:].unsqueeze(1).to_broadcast([P, TILES, D]), op=ALU.add,
+            )
+
+        def second_matmul(g):
+            for b in range(2):
+                o = psum_o.tile([P, 2, D], F32, name="o")
+                for jj in range(2):
+                    j = 2 * b + jj
+                    nc.tensor.matmul_mx(
+                        out=o[:, jj, :],
+                        lhsT=g_codes[g][0][:, j * P:(j + 1) * P].bitcast(FP8X4),
+                        lhsT_scale=g_codes[g][1][:, j * P:(j + 1) * P],
+                        rhs=w2_codes[:].bitcast(FP8X4),
+                        rhs_scale=w2_scales[:],
+                        start=True, stop=True,
+                    )
+                o_banks[(g, b)] = o
+
+        def residual(g):
+            y[g] = three.tile([P, TILES, D], F32, name="y")
+            stats[g] = (four.tile([P, TILES], F32, name="sums"),
+                        four.tile([P, TILES], F32, name="negmu"),
+                        four.tile([P, TILES], F32, name="ssq"),
+                        four.tile([P, TILES], F32, name="rstd"))
+            for j in range(TILES):
+                nc.vector.scalar_tensor_tensor(
+                    out=y[g][:, j, :], in0=o_banks[(g, j // 2)][:, j % 2, :], scalar=0.0,
+                    in1=xb[g][:, j, :], op0=ALU.add, op1=ALU.add,
+                    accum_out=stats[g][0][:, j:j + 1],
+                )
+            nc.vector.tensor_scalar_mul(out=stats[g][1][:], in0=stats[g][0][:], scalar1=-1.0 / D)
+
+        def variance(g):
+            for j in range(TILES):
+                junk = two.tile([P, D], BF16, name="junk")
+                nc.scalar.activation(out=junk[:], in_=y[g][:, j, :], func=ACT.Square,
+                                     bias=stats[g][1][:, j:j + 1], scale=1.0,
+                                     accum_out=stats[g][2][:, j:j + 1])
+            nc.gpsimd.tensor_scalar(out=stats[g][2][:], in0=stats[g][2][:], scalar1=1.0,
+                                    scalar2=D * LN_EPS, op0=ALU.mult, op1=ALU.add)
+            nc.gpsimd.tensor_tensor(out=stats[g][3][:], in0=stats[g][2][:], in1=minus_half[:],
+                                    op=ALU.pow)
+
+        def centre_and_gain(g):
+            res[g] = four.tile([P, TILES, D], F32, name="res")
+            for j in range(TILES):
+                nc.vector.scalar_tensor_tensor(
+                    out=res[g][:, j, :], in0=y[g][:, j, :], scalar=stats[g][1][:, j:j + 1],
+                    in1=ln_c[:, 0:D], op0=ALU.add, op1=ALU.mult,
+                )
+
+        def scale_and_shift(g):
+            for j in range(TILES - SCALAR_TILES):
+                nc.vector.scalar_tensor_tensor(
+                    out=res[g][:, j, :], in0=res[g][:, j, :], scalar=stats[g][3][:, j:j + 1],
+                    in1=ln_c[:, D:2 * D], op0=ALU.mult, op1=ALU.add,
+                )
+            for j in range(TILES - SCALAR_TILES, TILES):
+                nc.scalar.activation(out=res[g][:, j, :], in_=res[g][:, j, :], func=ACT.Copy,
+                                     scale=stats[g][3][:, j:j + 1])
+                nc.gpsimd.tensor_tensor(out=res[g][:, j, :], in0=res[g][:, j, :], in1=lnb_b[:],
+                                        op=ALU.add)
+            nc.sync.dma_start(out=out_view[g], in_=res[g][:])
+
+        def run(stage, g, first=0):
+            if first <= g < N_GROUPS:
+                stage(g)
+
+        transposes("w")
+        copies("w", ("scalar", "vector"))
+        quantise("w")
+        transposes(0)
+        copies(0, ("scalar", "vector"))
+        quantise(0)
+        transposes(1)
+        first_matmul(0)
+        constants()
+        copies(1, ("vector", "vector"))
+        quantise(1)
+        transposes(2)
+        first_matmul(1)
+        add_bias(0)
+        copies(2, ("vector", "vector"))
+        regroup(0)
+        quantise(2)
+        second_weight()
+        add_bias(1)
+
+        for i in range(-1, N_GROUPS + 1):
+            run(first_matmul, i + 2, 2)
+            run(copies, i + 3, 3)
+            run(regroup, i + 1, 1)
+            run(residual, i)
+            run(quantise_g, i + 1)
+            run(second_matmul, i + 1)
+            run(transposes, i + 4, 3)
+            run(variance, i)
+            run(centre_and_gain, i)
+            run(quantise, i + 3, 3)
+            run(scale_and_shift, i - 1)
+            run(add_bias, i + 2, 2)

@@ -20,7 +20,6 @@ GROUP = 512
 TILES = GROUP // P
 N_GROUPS = TOKENS // GROUP
 LN_EPS = 1e-5
-SCALAR_TILES = 0
 
 FLOPS = 2 * TOKENS * H * F + 2 * TOKENS * F * D
 
@@ -36,6 +35,7 @@ def tile_simplifiedretnet_pb_t_kernel(tc, h_ret, x, W1, b1, W2, b2, ln_g, ln_b, 
         two = ctx.enter_context(tc.tile_pool(name="two", bufs=2))
         three = ctx.enter_context(tc.tile_pool(name="three", bufs=3))
         four = ctx.enter_context(tc.tile_pool(name="four", bufs=4))
+        eight = ctx.enter_context(tc.tile_pool(name="eight", bufs=8))
         psum_t = ctx.enter_context(tc.psum_pool(name="psum_t", bufs=2))
         psum_z = ctx.enter_context(tc.psum_pool(name="psum_z", bufs=3))
         psum_o = ctx.enter_context(tc.psum_pool(name="psum_o", bufs=2))
@@ -83,7 +83,6 @@ def tile_simplifiedretnet_pb_t_kernel(tc, h_ret, x, W1, b1, W2, b2, ln_g, ln_b, 
         w2_scales = keep.tile([P, D], U8, name="w2_scales", align_bytes=64)
         ln_c = psum_c.tile([P, 2 * D], F32, name="ln_c")
         b2_b = keep.tile([P, D], F32, name="b2_b")
-        lnb_b = keep.tile([P, D], F32, name="lnb_b")
 
         banks = {}
         grouped = {}
@@ -117,7 +116,7 @@ def tile_simplifiedretnet_pb_t_kernel(tc, h_ret, x, W1, b1, W2, b2, ln_g, ln_b, 
                 banks[(key, b)] = tp
 
         def copies(key, engines=("scalar", "scalar")):
-            t = two.tile([P, 4 * GROUP], BF16, name="grouped", align_bytes=64)
+            t = three.tile([P, 4 * GROUP], BF16, name="grouped", align_bytes=64)
             grouped[key] = t
             words = t[:].bitcast(F32).rearrange("p (t u) -> p t u", u=2)
             for b in range(2):
@@ -150,8 +149,6 @@ def tile_simplifiedretnet_pb_t_kernel(tc, h_ret, x, W1, b1, W2, b2, ln_g, ln_b, 
             o = psum_o.tile([P, 2, D], F32, name="o")
             nc.tensor.matmul(out=o[:, 0, :], lhsT=ones[:], rhs=rows[:, 0:D], start=True, stop=True)
             nc.vector.tensor_copy(out=b2_b[:], in_=o[:, 0, :])
-            if SCALAR_TILES:
-                nc.vector.tensor_copy(out=lnb_b[:], in_=ln_c[:, D:2 * D])
 
         def first_matmul(g):
             planes[g] = two.tile([P, TILES, GROUP], BF16, name="planes")
@@ -182,11 +179,10 @@ def tile_simplifiedretnet_pb_t_kernel(tc, h_ret, x, W1, b1, W2, b2, ln_g, ln_b, 
                                   in_=g_grouped[g][:].rearrange("p w j -> p (w j)"))
 
         def add_bias(g):
-            xb[g] = four.tile([P, TILES, D], F32, name="xb")
-            nc.gpsimd.tensor_tensor(
-                out=xb[g][:], in0=x_sb[g][:],
-                in1=b2_b[:].unsqueeze(1).to_broadcast([P, TILES, D]), op=ALU.add,
-            )
+            for j in range(TILES):
+                xb[(g, j)] = eight.tile([P, D], F32, name="xb")
+                nc.gpsimd.tensor_tensor(out=xb[(g, j)][:], in0=x_sb[g][:, j, :], in1=b2_b[:],
+                                        op=ALU.add)
 
         def second_matmul(g):
             for b in range(2):
@@ -212,17 +208,19 @@ def tile_simplifiedretnet_pb_t_kernel(tc, h_ret, x, W1, b1, W2, b2, ln_g, ln_b, 
             for j in range(TILES):
                 nc.vector.scalar_tensor_tensor(
                     out=y[g][:, j, :], in0=o_banks[(g, j // 2)][:, j % 2, :], scalar=0.0,
-                    in1=xb[g][:, j, :], op0=ALU.add, op1=ALU.add,
+                    in1=xb[(g, j)][:], op0=ALU.add, op1=ALU.add,
                     accum_out=stats[g][0][:, j:j + 1],
                 )
-            nc.vector.tensor_scalar_mul(out=stats[g][1][:], in0=stats[g][0][:], scalar1=-1.0 / D)
 
         def variance(g):
+            nc.scalar.mul(out=stats[g][1][:], in_=stats[g][0][:], mul=-1.0 / D)
             for j in range(TILES):
                 junk = two.tile([P, D], BF16, name="junk")
                 nc.scalar.activation(out=junk[:], in_=y[g][:, j, :], func=ACT.Square,
                                      bias=stats[g][1][:, j:j + 1], scale=1.0,
                                      accum_out=stats[g][2][:, j:j + 1])
+
+        def inverse_deviation(g):
             nc.gpsimd.tensor_scalar(out=stats[g][2][:], in0=stats[g][2][:], scalar1=1.0,
                                     scalar2=D * LN_EPS, op0=ALU.mult, op1=ALU.add)
             nc.gpsimd.tensor_tensor(out=stats[g][3][:], in0=stats[g][2][:], in1=minus_half[:],
@@ -237,16 +235,11 @@ def tile_simplifiedretnet_pb_t_kernel(tc, h_ret, x, W1, b1, W2, b2, ln_g, ln_b, 
                 )
 
         def scale_and_shift(g):
-            for j in range(TILES - SCALAR_TILES):
+            for j in range(TILES):
                 nc.vector.scalar_tensor_tensor(
                     out=res[g][:, j, :], in0=res[g][:, j, :], scalar=stats[g][3][:, j:j + 1],
                     in1=ln_c[:, D:2 * D], op0=ALU.mult, op1=ALU.add,
                 )
-            for j in range(TILES - SCALAR_TILES, TILES):
-                nc.scalar.activation(out=res[g][:, j, :], in_=res[g][:, j, :], func=ACT.Copy,
-                                     scale=stats[g][3][:, j:j + 1])
-                nc.gpsimd.tensor_tensor(out=res[g][:, j, :], in0=res[g][:, j, :], in1=lnb_b[:],
-                                        op=ALU.add)
             nc.sync.dma_start(out=out_view[g], in_=res[g][:])
 
         def run(stage, g, first=0):
@@ -272,17 +265,21 @@ def tile_simplifiedretnet_pb_t_kernel(tc, h_ret, x, W1, b1, W2, b2, ln_g, ln_b, 
         quantise(2)
         second_weight()
         add_bias(1)
+        transposes(3)
+        copies(3, ("vector", "vector"))
+        transposes(4)
 
         for i in range(-1, N_GROUPS + 1):
             run(first_matmul, i + 2, 2)
-            run(copies, i + 3, 3)
+            run(copies, i + 4, 4)
             run(regroup, i + 1, 1)
-            run(residual, i)
+            run(quantise, i + 3, 3)
             run(quantise_g, i + 1)
             run(second_matmul, i + 1)
-            run(transposes, i + 4, 3)
+            run(transposes, i + 5, 5)
+            run(residual, i)
             run(variance, i)
-            run(centre_and_gain, i)
-            run(quantise, i + 3, 3)
-            run(scale_and_shift, i - 1)
+            run(inverse_deviation, i - 1)
             run(add_bias, i + 2, 2)
+            run(scale_and_shift, i - 1)
+            run(centre_and_gain, i)

@@ -20,6 +20,7 @@ GROUP = 512
 TILES = GROUP // P
 N_GROUPS = TOKENS // GROUP
 LN_EPS = 1e-5
+POOL_TILES = 2
 
 FLOPS = 2 * TOKENS * H * F + 2 * TOKENS * F * D
 
@@ -35,7 +36,7 @@ def tile_simplifiedretnet_pb_t_kernel(tc, h_ret, x, W1, b1, W2, b2, ln_g, ln_b, 
         two = ctx.enter_context(tc.tile_pool(name="two", bufs=2))
         three = ctx.enter_context(tc.tile_pool(name="three", bufs=3))
         four = ctx.enter_context(tc.tile_pool(name="four", bufs=4))
-        eight = ctx.enter_context(tc.tile_pool(name="eight", bufs=8))
+        six = ctx.enter_context(tc.tile_pool(name="six", bufs=6))
         psum_t = ctx.enter_context(tc.psum_pool(name="psum_t", bufs=2))
         psum_z = ctx.enter_context(tc.psum_pool(name="psum_z", bufs=3))
         psum_o = ctx.enter_context(tc.psum_pool(name="psum_o", bufs=2))
@@ -179,9 +180,15 @@ def tile_simplifiedretnet_pb_t_kernel(tc, h_ret, x, W1, b1, W2, b2, ln_g, ln_b, 
                                   in_=g_grouped[g][:].rearrange("p w j -> p (w j)"))
 
         def add_bias(g):
-            for j in range(TILES):
-                xb[(g, j)] = eight.tile([P, D], F32, name="xb")
+            for j in range(POOL_TILES):
+                xb[(g, j)] = four.tile([P, D], F32, name="xb")
                 nc.gpsimd.tensor_tensor(out=xb[(g, j)][:], in0=x_sb[g][:, j, :], in1=b2_b[:],
+                                        op=ALU.add)
+
+        def add_bias_on_vector(g):
+            for j in range(POOL_TILES, TILES):
+                xb[(g, j)] = six.tile([P, D], F32, name="xbv")
+                nc.vector.tensor_tensor(out=xb[(g, j)][:], in0=x_sb[g][:, j, :], in1=b2_b[:],
                                         op=ALU.add)
 
         def second_matmul(g):
@@ -260,11 +267,13 @@ def tile_simplifiedretnet_pb_t_kernel(tc, h_ret, x, W1, b1, W2, b2, ln_g, ln_b, 
         transposes(2)
         first_matmul(1)
         add_bias(0)
+        add_bias_on_vector(0)
         copies(2, ("vector", "vector"))
         regroup(0)
         quantise(2)
         second_weight()
         add_bias(1)
+        add_bias_on_vector(1)
         transposes(3)
         copies(3, ("vector", "vector"))
         transposes(4)
@@ -275,6 +284,7 @@ def tile_simplifiedretnet_pb_t_kernel(tc, h_ret, x, W1, b1, W2, b2, ln_g, ln_b, 
             run(regroup, i + 1, 1)
             run(quantise, i + 3, 3)
             run(quantise_g, i + 1)
+            run(add_bias_on_vector, i + 2, 2)
             run(second_matmul, i + 1)
             run(transposes, i + 5, 5)
             run(residual, i)

@@ -20,7 +20,6 @@ GROUP = 512
 TILES = GROUP // P
 N_GROUPS = TOKENS // GROUP
 LN_EPS = 1e-5
-POOL_TILES = 2
 
 FLOPS = 2 * TOKENS * H * F + 2 * TOKENS * F * D
 
@@ -36,7 +35,7 @@ def tile_simplifiedretnet_pb_t_kernel(tc, h_ret, x, W1, b1, W2, b2, ln_g, ln_b, 
         two = ctx.enter_context(tc.tile_pool(name="two", bufs=2))
         three = ctx.enter_context(tc.tile_pool(name="three", bufs=3))
         four = ctx.enter_context(tc.tile_pool(name="four", bufs=4))
-        six = ctx.enter_context(tc.tile_pool(name="six", bufs=6))
+        eight = ctx.enter_context(tc.tile_pool(name="eight", bufs=8))
         psum_t = ctx.enter_context(tc.psum_pool(name="psum_t", bufs=2))
         psum_z = ctx.enter_context(tc.psum_pool(name="psum_z", bufs=3))
         psum_o = ctx.enter_context(tc.psum_pool(name="psum_o", bufs=2))
@@ -84,6 +83,7 @@ def tile_simplifiedretnet_pb_t_kernel(tc, h_ret, x, W1, b1, W2, b2, ln_g, ln_b, 
         w2_scales = keep.tile([P, D], U8, name="w2_scales", align_bytes=64)
         ln_c = psum_c.tile([P, 2 * D], F32, name="ln_c")
         b2_b = keep.tile([P, D], F32, name="b2_b")
+        ln_s = keep.tile([P, 2 * D], F32, name="ln_s")
 
         banks = {}
         grouped = {}
@@ -150,6 +150,7 @@ def tile_simplifiedretnet_pb_t_kernel(tc, h_ret, x, W1, b1, W2, b2, ln_g, ln_b, 
             o = psum_o.tile([P, 2, D], F32, name="o")
             nc.tensor.matmul(out=o[:, 0, :], lhsT=ones[:], rhs=rows[:, 0:D], start=True, stop=True)
             nc.vector.tensor_copy(out=b2_b[:], in_=o[:, 0, :])
+            nc.vector.tensor_copy(out=ln_s[:], in_=ln_c[:])
 
         def first_matmul(g):
             planes[g] = two.tile([P, TILES, GROUP], BF16, name="planes")
@@ -180,15 +181,9 @@ def tile_simplifiedretnet_pb_t_kernel(tc, h_ret, x, W1, b1, W2, b2, ln_g, ln_b, 
                                   in_=g_grouped[g][:].rearrange("p w j -> p (w j)"))
 
         def add_bias(g):
-            for j in range(POOL_TILES):
-                xb[(g, j)] = four.tile([P, D], F32, name="xb")
+            for j in range(TILES):
+                xb[(g, j)] = eight.tile([P, D], F32, name="xb")
                 nc.gpsimd.tensor_tensor(out=xb[(g, j)][:], in0=x_sb[g][:, j, :], in1=b2_b[:],
-                                        op=ALU.add)
-
-        def add_bias_on_vector(g):
-            for j in range(POOL_TILES, TILES):
-                xb[(g, j)] = six.tile([P, D], F32, name="xbv")
-                nc.vector.tensor_tensor(out=xb[(g, j)][:], in0=x_sb[g][:, j, :], in1=b2_b[:],
                                         op=ALU.add)
 
         def second_matmul(g):
@@ -238,14 +233,14 @@ def tile_simplifiedretnet_pb_t_kernel(tc, h_ret, x, W1, b1, W2, b2, ln_g, ln_b, 
             for j in range(TILES):
                 nc.vector.scalar_tensor_tensor(
                     out=res[g][:, j, :], in0=y[g][:, j, :], scalar=stats[g][1][:, j:j + 1],
-                    in1=ln_c[:, 0:D], op0=ALU.add, op1=ALU.mult,
+                    in1=ln_s[:, 0:D], op0=ALU.add, op1=ALU.mult,
                 )
 
         def scale_and_shift(g):
             for j in range(TILES):
                 nc.vector.scalar_tensor_tensor(
                     out=res[g][:, j, :], in0=res[g][:, j, :], scalar=stats[g][3][:, j:j + 1],
-                    in1=ln_c[:, D:2 * D], op0=ALU.mult, op1=ALU.add,
+                    in1=ln_s[:, D:2 * D], op0=ALU.mult, op1=ALU.add,
                 )
             nc.sync.dma_start(out=out_view[g], in_=res[g][:])
 
@@ -267,13 +262,11 @@ def tile_simplifiedretnet_pb_t_kernel(tc, h_ret, x, W1, b1, W2, b2, ln_g, ln_b, 
         transposes(2)
         first_matmul(1)
         add_bias(0)
-        add_bias_on_vector(0)
         copies(2, ("vector", "vector"))
         regroup(0)
         quantise(2)
         second_weight()
         add_bias(1)
-        add_bias_on_vector(1)
         transposes(3)
         copies(3, ("vector", "vector"))
         transposes(4)
@@ -284,7 +277,6 @@ def tile_simplifiedretnet_pb_t_kernel(tc, h_ret, x, W1, b1, W2, b2, ln_g, ln_b, 
             run(regroup, i + 1, 1)
             run(quantise, i + 3, 3)
             run(quantise_g, i + 1)
-            run(add_bias_on_vector, i + 2, 2)
             run(second_matmul, i + 1)
             run(transposes, i + 5, 5)
             run(residual, i)

@@ -20,6 +20,8 @@ GROUP = 512
 TILES = GROUP // P
 N_GROUPS = TOKENS // GROUP
 LN_EPS = 1e-5
+POOL_TILES = 3
+SCALAR_TOKENS = 256
 
 FLOPS = 2 * TOKENS * H * F + 2 * TOKENS * F * D
 
@@ -35,7 +37,8 @@ def tile_simplifiedretnet_pb_t_kernel(tc, h_ret, x, W1, b1, W2, b2, ln_g, ln_b, 
         two = ctx.enter_context(tc.tile_pool(name="two", bufs=2))
         three = ctx.enter_context(tc.tile_pool(name="three", bufs=3))
         four = ctx.enter_context(tc.tile_pool(name="four", bufs=4))
-        eight = ctx.enter_context(tc.tile_pool(name="eight", bufs=8))
+        xb_pool = ctx.enter_context(tc.tile_pool(name="xb_pool", bufs=2 * POOL_TILES))
+        xbv_pool = ctx.enter_context(tc.tile_pool(name="xbv_pool", bufs=3 * (TILES - POOL_TILES)))
         psum_t = ctx.enter_context(tc.psum_pool(name="psum_t", bufs=2))
         psum_z = ctx.enter_context(tc.psum_pool(name="psum_z", bufs=3))
         psum_o = ctx.enter_context(tc.psum_pool(name="psum_o", bufs=2))
@@ -83,7 +86,6 @@ def tile_simplifiedretnet_pb_t_kernel(tc, h_ret, x, W1, b1, W2, b2, ln_g, ln_b, 
         w2_scales = keep.tile([P, D], U8, name="w2_scales", align_bytes=64)
         ln_c = psum_c.tile([P, 2 * D], F32, name="ln_c")
         b2_b = keep.tile([P, D], F32, name="b2_b")
-        ln_s = keep.tile([P, 2 * D], F32, name="ln_s")
 
         banks = {}
         grouped = {}
@@ -150,7 +152,6 @@ def tile_simplifiedretnet_pb_t_kernel(tc, h_ret, x, W1, b1, W2, b2, ln_g, ln_b, 
             o = psum_o.tile([P, 2, D], F32, name="o")
             nc.tensor.matmul(out=o[:, 0, :], lhsT=ones[:], rhs=rows[:, 0:D], start=True, stop=True)
             nc.vector.tensor_copy(out=b2_b[:], in_=o[:, 0, :])
-            nc.vector.tensor_copy(out=ln_s[:], in_=ln_c[:])
 
         def first_matmul(g):
             planes[g] = two.tile([P, TILES, GROUP], BF16, name="planes")
@@ -167,11 +168,19 @@ def tile_simplifiedretnet_pb_t_kernel(tc, h_ret, x, W1, b1, W2, b2, ln_g, ln_b, 
                 nc.scalar.activation(out=planes[g][:, c, :], in_=z[:], func=ACT.Gelu,
                                      bias=b1_c[:, c:c + 1], scale=1.0)
 
+        def regroup_on_scalar(g):
+            g_grouped[g] = three.tile([P, GROUP, 4], BF16, name="g_grouped", align_bytes=64)
+            cut = GROUP - SCALAR_TOKENS
+            nc.scalar.copy(
+                out=g_grouped[g][:, cut:, :].rearrange("p (c i) t -> p c t i", i=4),
+                in_=planes[g][:, :, cut:].rearrange("p t (c i) -> p c t i", i=4),
+            )
+
         def regroup(g):
-            g_grouped[g] = two.tile([P, GROUP, 4], BF16, name="g_grouped", align_bytes=64)
+            cut = GROUP - SCALAR_TOKENS
             nc.vector.tensor_copy(
-                out=g_grouped[g][:].rearrange("p (c i) t -> p c t i", i=4),
-                in_=planes[g][:].rearrange("p t (c i) -> p c t i", i=4),
+                out=g_grouped[g][:, :cut, :].rearrange("p (c i) t -> p c t i", i=4),
+                in_=planes[g][:, :, :cut].rearrange("p t (c i) -> p c t i", i=4),
             )
 
         def quantise_g(g):
@@ -181,9 +190,15 @@ def tile_simplifiedretnet_pb_t_kernel(tc, h_ret, x, W1, b1, W2, b2, ln_g, ln_b, 
                                   in_=g_grouped[g][:].rearrange("p w j -> p (w j)"))
 
         def add_bias(g):
-            for j in range(TILES):
-                xb[(g, j)] = eight.tile([P, D], F32, name="xb")
+            for j in range(POOL_TILES):
+                xb[(g, j)] = xb_pool.tile([P, D], F32, name="xb")
                 nc.gpsimd.tensor_tensor(out=xb[(g, j)][:], in0=x_sb[g][:, j, :], in1=b2_b[:],
+                                        op=ALU.add)
+
+        def add_bias_on_vector(g):
+            for j in range(POOL_TILES, TILES):
+                xb[(g, j)] = xbv_pool.tile([P, D], F32, name="xbv")
+                nc.vector.tensor_tensor(out=xb[(g, j)][:], in0=x_sb[g][:, j, :], in1=b2_b[:],
                                         op=ALU.add)
 
         def second_matmul(g):
@@ -233,14 +248,14 @@ def tile_simplifiedretnet_pb_t_kernel(tc, h_ret, x, W1, b1, W2, b2, ln_g, ln_b, 
             for j in range(TILES):
                 nc.vector.scalar_tensor_tensor(
                     out=res[g][:, j, :], in0=y[g][:, j, :], scalar=stats[g][1][:, j:j + 1],
-                    in1=ln_s[:, 0:D], op0=ALU.add, op1=ALU.mult,
+                    in1=ln_c[:, 0:D], op0=ALU.add, op1=ALU.mult,
                 )
 
         def scale_and_shift(g):
             for j in range(TILES):
                 nc.vector.scalar_tensor_tensor(
                     out=res[g][:, j, :], in0=res[g][:, j, :], scalar=stats[g][3][:, j:j + 1],
-                    in1=ln_s[:, D:2 * D], op0=ALU.mult, op1=ALU.add,
+                    in1=ln_c[:, D:2 * D], op0=ALU.mult, op1=ALU.add,
                 )
             nc.sync.dma_start(out=out_view[g], in_=res[g][:])
 
@@ -256,17 +271,21 @@ def tile_simplifiedretnet_pb_t_kernel(tc, h_ret, x, W1, b1, W2, b2, ln_g, ln_b, 
         quantise(0)
         transposes(1)
         first_matmul(0)
+        regroup_on_scalar(0)
         constants()
         copies(1, ("vector", "vector"))
         quantise(1)
         transposes(2)
         first_matmul(1)
+        regroup_on_scalar(1)
         add_bias(0)
+        add_bias_on_vector(0)
         copies(2, ("vector", "vector"))
         regroup(0)
         quantise(2)
         second_weight()
         add_bias(1)
+        add_bias_on_vector(1)
         transposes(3)
         copies(3, ("vector", "vector"))
         transposes(4)
@@ -274,9 +293,11 @@ def tile_simplifiedretnet_pb_t_kernel(tc, h_ret, x, W1, b1, W2, b2, ln_g, ln_b, 
         for i in range(-1, N_GROUPS + 1):
             run(first_matmul, i + 2, 2)
             run(copies, i + 4, 4)
+            run(regroup_on_scalar, i + 2, 2)
             run(regroup, i + 1, 1)
             run(quantise, i + 3, 3)
             run(quantise_g, i + 1)
+            run(add_bias_on_vector, i + 2, 2)
             run(second_matmul, i + 1)
             run(transposes, i + 5, 5)
             run(residual, i)

@@ -22,6 +22,8 @@ N_GROUPS = TOKENS // GROUP
 LN_EPS = 1e-5
 POOL_TILES = 3
 SCALAR_TOKENS = 256
+Z_BANKS = 3
+EARLY_GROUPS = 5
 
 FLOPS = 2 * TOKENS * H * F + 2 * TOKENS * F * D
 
@@ -40,7 +42,7 @@ def tile_simplifiedretnet_pb_t_kernel(tc, h_ret, x, W1, b1, W2, b2, ln_g, ln_b, 
         xb_pool = ctx.enter_context(tc.tile_pool(name="xb_pool", bufs=2 * POOL_TILES))
         xbv_pool = ctx.enter_context(tc.tile_pool(name="xbv_pool", bufs=3 * (TILES - POOL_TILES)))
         psum_t = ctx.enter_context(tc.psum_pool(name="psum_t", bufs=2))
-        psum_z = ctx.enter_context(tc.psum_pool(name="psum_z", bufs=3))
+        psum_z = ctx.enter_context(tc.psum_pool(name="psum_z", bufs=Z_BANKS))
         psum_o = ctx.enter_context(tc.psum_pool(name="psum_o", bufs=2))
         psum_c = ctx.enter_context(tc.psum_pool(name="psum_c", bufs=1))
         ctx.enter_context(tc.manual_schedule())
@@ -91,6 +93,7 @@ def tile_simplifiedretnet_pb_t_kernel(tc, h_ret, x, W1, b1, W2, b2, ln_g, ln_b, 
         grouped = {}
         codes = {"w": (w1_codes, w1_scales)}
         planes = {}
+        z_banks = {}
         g_grouped = {}
         g_codes = {}
         o_banks = {}
@@ -118,7 +121,9 @@ def tile_simplifiedretnet_pb_t_kernel(tc, h_ret, x, W1, b1, W2, b2, ln_g, ln_b, 
                         )
                 banks[(key, b)] = tp
 
-        def copies(key, engines=("scalar", "scalar")):
+        def copies(key, engines=None):
+            if engines is None:
+                engines = ("vector", "vector") if key < EARLY_GROUPS else ("scalar", "scalar")
             t = three.tile([P, 4 * GROUP], BF16, name="grouped", align_bytes=64)
             grouped[key] = t
             words = t[:].bitcast(F32).rearrange("p (t u) -> p t u", u=2)
@@ -128,14 +133,14 @@ def tile_simplifiedretnet_pb_t_kernel(tc, h_ret, x, W1, b1, W2, b2, ln_g, ln_b, 
 
         def quantise(key):
             if key != "w":
-                codes[key] = (three.tile([P, GROUP], U32, name="h_codes", align_bytes=64),
-                              three.tile([P, GROUP], U8, name="h_scales", align_bytes=64))
+                codes[key] = (four.tile([P, GROUP], U32, name="h_codes", align_bytes=64),
+                              four.tile([P, GROUP], U8, name="h_scales", align_bytes=64))
             nc.vector.quantize_mx(out=codes[key][0][:].bitcast(FP8X4), scales=codes[key][1][:],
                                   in_=grouped[key][:])
 
         def second_weight():
             words = w2_sb[:].bitcast(F32).rearrange("p a (q u) -> p a q u", u=2)
-            tp = psum_t.tile([P, 2, 2 * P], F32, name="tp")
+            tp = psum_o.tile([P, 2, D], F32, name="o")
             for a in range(2):
                 for u in range(2):
                     nc.tensor.transpose(tp[:, u, a * P:(a + 1) * P], words[:, a, :, u], ident[:])
@@ -153,20 +158,27 @@ def tile_simplifiedretnet_pb_t_kernel(tc, h_ret, x, W1, b1, W2, b2, ln_g, ln_b, 
             nc.tensor.matmul(out=o[:, 0, :], lhsT=ones[:], rhs=rows[:, 0:D], start=True, stop=True)
             nc.vector.tensor_copy(out=b2_b[:], in_=o[:, 0, :])
 
-        def first_matmul(g):
+        def first_pass(n):
+            g, c = n // TILES, n % TILES
+            z = psum_z.tile([P, GROUP], F32, name="z")
+            nc.tensor.matmul_mx(
+                out=z[:],
+                lhsT=w1_codes[:, c * P:(c + 1) * P].bitcast(FP8X4),
+                lhsT_scale=w1_scales[:, c * P:(c + 1) * P],
+                rhs=codes[g][0][:].bitcast(FP8X4),
+                rhs_scale=codes[g][1][:],
+                start=True, stop=True,
+            )
+            z_banks[n] = z
+
+        def gelu(g):
             planes[g] = two.tile([P, TILES, GROUP], BF16, name="planes")
             for c in range(TILES):
-                z = psum_z.tile([P, GROUP], F32, name="z")
-                nc.tensor.matmul_mx(
-                    out=z[:],
-                    lhsT=w1_codes[:, c * P:(c + 1) * P].bitcast(FP8X4),
-                    lhsT_scale=w1_scales[:, c * P:(c + 1) * P],
-                    rhs=codes[g][0][:].bitcast(FP8X4),
-                    rhs_scale=codes[g][1][:],
-                    start=True, stop=True,
-                )
-                nc.scalar.activation(out=planes[g][:, c, :], in_=z[:], func=ACT.Gelu,
+                n = TILES * g + c
+                nc.scalar.activation(out=planes[g][:, c, :], in_=z_banks[n][:], func=ACT.Gelu,
                                      bias=b1_c[:, c:c + 1], scale=1.0)
+                if n + Z_BANKS < TILES * N_GROUPS:
+                    first_pass(n + Z_BANKS)
 
         def regroup_on_scalar(g):
             g_grouped[g] = three.tile([P, GROUP, 4], BF16, name="g_grouped", align_bytes=64)
@@ -257,7 +269,10 @@ def tile_simplifiedretnet_pb_t_kernel(tc, h_ret, x, W1, b1, W2, b2, ln_g, ln_b, 
                     out=res[g][:, j, :], in0=res[g][:, j, :], scalar=stats[g][3][:, j:j + 1],
                     in1=ln_c[:, D:2 * D], op0=ALU.mult, op1=ALU.add,
                 )
-            nc.sync.dma_start(out=out_view[g], in_=res[g][:])
+                if g == N_GROUPS - 1:
+                    nc.sync.dma_start(out=out_view[g][:, j, :], in_=res[g][:, j, :])
+            if g < N_GROUPS - 1:
+                nc.sync.dma_start(out=out_view[g], in_=res[g][:])
 
         def run(stage, g, first=0):
             if first <= g < N_GROUPS:
@@ -270,36 +285,30 @@ def tile_simplifiedretnet_pb_t_kernel(tc, h_ret, x, W1, b1, W2, b2, ln_g, ln_b, 
         copies(0, ("scalar", "vector"))
         quantise(0)
         transposes(1)
-        first_matmul(0)
-        regroup_on_scalar(0)
-        constants()
-        copies(1, ("vector", "vector"))
+        for n in range(Z_BANKS):
+            first_pass(n)
+        copies(1)
         quantise(1)
-        transposes(2)
-        first_matmul(1)
-        regroup_on_scalar(1)
-        add_bias(0)
-        add_bias_on_vector(0)
-        copies(2, ("vector", "vector"))
-        regroup(0)
-        quantise(2)
+        constants()
         second_weight()
-        add_bias(1)
-        add_bias_on_vector(1)
+        transposes(2)
+        for g in range(2):
+            add_bias(g)
+            add_bias_on_vector(g)
+        gelu(0)
+        copies(2)
         transposes(3)
-        copies(3, ("vector", "vector"))
-        transposes(4)
 
-        for i in range(-1, N_GROUPS + 1):
-            run(first_matmul, i + 2, 2)
-            run(copies, i + 4, 4)
-            run(regroup_on_scalar, i + 2, 2)
-            run(regroup, i + 1, 1)
-            run(quantise, i + 3, 3)
+        for i in range(-2, N_GROUPS + 1):
+            run(gelu, i + 2, 1)
+            run(copies, i + 5, 3)
+            run(transposes, i + 6, 4)
+            run(regroup_on_scalar, i + 2)
+            run(regroup, i + 1)
+            run(quantise, i + 4, 2)
             run(quantise_g, i + 1)
             run(add_bias_on_vector, i + 2, 2)
             run(second_matmul, i + 1)
-            run(transposes, i + 5, 5)
             run(residual, i)
             run(variance, i)
             run(inverse_deviation, i - 1)

@@ -249,9 +249,11 @@ def tile_simplifiedretnet_pb_t_kernel(tc, h_ret, x, W1, b1, W2, b2, ln_g, ln_b, 
                                      bias=stats[g][1][:, j:j + 1], scale=1.0,
                                      accum_out=stats[g][2][:, j:j + 1])
 
+        def add_eps(g):
+            nc.vector.tensor_scalar_add(out=stats[g][2][:], in0=stats[g][2][:],
+                                        scalar1=D * LN_EPS)
+
         def inverse_deviation(g):
-            nc.gpsimd.tensor_scalar(out=stats[g][2][:], in0=stats[g][2][:], scalar1=1.0,
-                                    scalar2=D * LN_EPS, op0=ALU.mult, op1=ALU.add)
             nc.gpsimd.tensor_tensor(out=stats[g][3][:], in0=stats[g][2][:], in1=minus_half[:],
                                     op=ALU.pow)
 
@@ -292,9 +294,8 @@ def tile_simplifiedretnet_pb_t_kernel(tc, h_ret, x, W1, b1, W2, b2, ln_g, ln_b, 
         constants()
         second_weight()
         transposes(2)
-        for g in range(2):
-            add_bias(g)
-            add_bias_on_vector(g)
+        add_bias(0)
+        add_bias_on_vector(0)
         gelu(0)
         copies(2)
         transposes(3)
@@ -305,13 +306,14 @@ def tile_simplifiedretnet_pb_t_kernel(tc, h_ret, x, W1, b1, W2, b2, ln_g, ln_b, 
             run(transposes, i + 6, 4)
             run(regroup_on_scalar, i + 2)
             run(regroup, i + 1)
+            run(add_eps, i - 1)
             run(quantise, i + 4, 2)
             run(quantise_g, i + 1)
-            run(add_bias_on_vector, i + 2, 2)
+            run(add_bias_on_vector, i + 2, 1)
             run(second_matmul, i + 1)
             run(residual, i)
             run(variance, i)
             run(inverse_deviation, i - 1)
-            run(add_bias, i + 2, 2)
+            run(add_bias, i + 2, 1)
             run(scale_and_shift, i - 1)
             run(centre_and_gain, i)

@@ -20,10 +20,9 @@ GROUP = 512
 TILES = GROUP // P
 N_GROUPS = TOKENS // GROUP
 LN_EPS = 1e-5
-POOL_TILES = 3
-SCALAR_TOKENS = 256
-Z_BANKS = 3
-EARLY_GROUPS = 5
+POOL_TOKENS = 320
+SCALAR_TOKENS = 64
+EARLY_GROUPS = 2
 
 FLOPS = 2 * TOKENS * H * F + 2 * TOKENS * F * D
 
@@ -39,29 +38,30 @@ def tile_simplifiedretnet_pb_t_kernel(tc, h_ret, x, W1, b1, W2, b2, ln_g, ln_b, 
         two = ctx.enter_context(tc.tile_pool(name="two", bufs=2))
         three = ctx.enter_context(tc.tile_pool(name="three", bufs=3))
         four = ctx.enter_context(tc.tile_pool(name="four", bufs=4))
-        xb_pool = ctx.enter_context(tc.tile_pool(name="xb_pool", bufs=2 * POOL_TILES))
-        xbv_pool = ctx.enter_context(tc.tile_pool(name="xbv_pool", bufs=3 * (TILES - POOL_TILES)))
         psum_t = ctx.enter_context(tc.psum_pool(name="psum_t", bufs=2))
-        psum_z = ctx.enter_context(tc.psum_pool(name="psum_z", bufs=Z_BANKS))
-        psum_o = ctx.enter_context(tc.psum_pool(name="psum_o", bufs=2))
+        psum_z = ctx.enter_context(tc.psum_pool(name="psum_z", bufs=2))
+        psum_o = ctx.enter_context(tc.psum_pool(name="psum_o", bufs=1))
+        psum_y = ctx.enter_context(tc.psum_pool(name="psum_y", bufs=2))
         psum_c = ctx.enter_context(tc.psum_pool(name="psum_c", bufs=1))
         ctx.enter_context(tc.manual_schedule())
 
         ident = keep.tile([P, P], F32, name="ident")
         make_identity(nc, ident[:])
-        rows = keep.tile([P, 3 * D], BF16, name="rows")
+        rows = keep.tile([P, 2 * D], BF16, name="rows")
         nc.vector.memset(rows[:], 0.0)
         ones = keep.tile([P, P], BF16, name="ones")
         nc.vector.memset(ones[:], 1.0)
-        sixteens = keep.tile([P, P], BF16, name="sixteens")
-        nc.vector.memset(sixteens[:], 16.0)
         minus_half = keep.tile([P, TILES], F32, name="minus_half")
         nc.vector.memset(minus_half[:], -0.5)
+        ident_b = keep.tile([P, P], BF16, name="ident_b")
+        nc.vector.tensor_copy(out=ident_b[:], in_=ident[:])
         b1_c = keep.tile([P, TILES], BF16, name="b1_c")
+        b2_c = keep.tile([P, 2], BF16, name="b2_c")
         nc.scalar.dma_start(out=b1_c[:], in_=b1.rearrange("(m c) -> m c", c=TILES))
-        nc.scalar.dma_start(out=rows[0:1, 0:D], in_=b2.rearrange("(o d) -> o d", o=1))
-        nc.scalar.dma_start(out=rows[0:1, D:2 * D], in_=ln_g.rearrange("(o d) -> o d", o=1))
-        nc.scalar.dma_start(out=rows[0:1, 2 * D:3 * D], in_=ln_b.rearrange("(o d) -> o d", o=1))
+        nc.scalar.dma_start(out=rows[0:1, 0:D], in_=ln_g.rearrange("(o d) -> o d", o=1))
+        nc.scalar.dma_start(out=rows[0:1, D:2 * D], in_=ln_b.rearrange("(o d) -> o d", o=1))
+        with nc.allow_non_contiguous_dma("128 pieces of two bytes a half"):
+            nc.scalar.dma_start(out=b2_c[:], in_=b2.rearrange("(a p) -> p a", p=P))
 
         w1_sb = keep.tile([P, TILES, H], BF16, name="w1_sb")
         w2_sb = keep.tile([P, 2, F], BF16, name="w2_sb")
@@ -75,19 +75,18 @@ def tile_simplifiedretnet_pb_t_kernel(tc, h_ret, x, W1, b1, W2, b2, ln_g, ln_b, 
         nc.sync.dma_start(out=src[1][:], in_=h_view[1])
         nc.sync.dma_start(out=w2_sb[:], in_=W2.rearrange("(a p) f -> p a f", p=P))
         nc.sync.dma_start(out=src[2][:], in_=h_view[2])
-        nc.sync.dma_start(out=x_sb[0][:], in_=x_view[0])
         nc.sync.dma_start(out=src[3][:], in_=h_view[3])
-        for g in range(1, N_GROUPS):
-            if g + 3 < N_GROUPS:
-                nc.sync.dma_start(out=src[g + 3][:], in_=h_view[g + 3])
+        for g in range(N_GROUPS):
             nc.sync.dma_start(out=x_sb[g][:], in_=x_view[g])
+            if g + 4 < N_GROUPS:
+                nc.sync.dma_start(out=src[g + 4][:], in_=h_view[g + 4])
 
         w1_codes = keep.tile([P, F], U32, name="w1_codes", align_bytes=64)
         w1_scales = keep.tile([P, F], U8, name="w1_scales", align_bytes=64)
         w2_codes = keep.tile([P, D], U32, name="w2_codes", align_bytes=64)
         w2_scales = keep.tile([P, D], U8, name="w2_scales", align_bytes=64)
-        ln_c = psum_c.tile([P, 2 * D], F32, name="ln_c")
-        b2_b = keep.tile([P, D], F32, name="b2_b")
+        ln_b_bank = psum_c.tile([P, 2 * D], F32, name="ln_b_bank")
+        ln_g_b = keep.tile([P, D], F32, name="ln_g_b")
 
         banks = {}
         grouped = {}
@@ -97,20 +96,14 @@ def tile_simplifiedretnet_pb_t_kernel(tc, h_ret, x, W1, b1, W2, b2, ln_g, ln_b, 
         g_grouped = {}
         g_codes = {}
         o_banks = {}
-        xb = {}
-        y = {}
+        o_t = {}
+        y_banks = {}
+        moments = {}
         res = {}
-        stats = {}
 
-        def copy_out(engine, dst, source):
-            if engine == "vector":
-                nc.vector.tensor_copy(out=dst, in_=source)
-            else:
-                nc.scalar.copy(out=dst, in_=source)
-
-        def transposes(key):
+        def transposes(key, halves=(0, 1)):
             words = src[key][:].bitcast(F32)
-            for b in range(2):
+            for b in halves:
                 tp = psum_t.tile([P, 2, 2 * P], F32, name="tp")
                 for jj in range(2):
                     for u in range(2):
@@ -121,15 +114,16 @@ def tile_simplifiedretnet_pb_t_kernel(tc, h_ret, x, W1, b1, W2, b2, ln_g, ln_b, 
                         )
                 banks[(key, b)] = tp
 
-        def copies(key, engines=None):
-            if engines is None:
-                engines = ("vector", "vector") if key < EARLY_GROUPS else ("scalar", "scalar")
-            t = three.tile([P, 4 * GROUP], BF16, name="grouped", align_bytes=64)
-            grouped[key] = t
-            words = t[:].bitcast(F32).rearrange("p (t u) -> p t u", u=2)
-            for b in range(2):
-                copy_out(engines[b], words[:, b * 2 * P:(b + 1) * 2 * P, :],
-                         banks[(key, b)][:].rearrange("p u t -> p t u"))
+        def copy_half(key, b, engine="scalar"):
+            if b == 0:
+                grouped[key] = three.tile([P, 4 * GROUP], BF16, name="grouped", align_bytes=64)
+            words = grouped[key][:].bitcast(F32).rearrange("p (t u) -> p t u", u=2)
+            dst = words[:, b * 2 * P:(b + 1) * 2 * P, :]
+            source = banks[(key, b)][:].rearrange("p u t -> p t u")
+            if engine == "vector":
+                nc.vector.tensor_copy(out=dst, in_=source)
+            else:
+                nc.scalar.copy(out=dst, in_=source)
 
         def quantise(key):
             if key != "w":
@@ -140,7 +134,7 @@ def tile_simplifiedretnet_pb_t_kernel(tc, h_ret, x, W1, b1, W2, b2, ln_g, ln_b, 
 
         def second_weight():
             words = w2_sb[:].bitcast(F32).rearrange("p a (q u) -> p a q u", u=2)
-            tp = psum_o.tile([P, 2, D], F32, name="o")
+            tp = psum_y.tile([P, 2, D], F32, name="y")
             for a in range(2):
                 for u in range(2):
                     nc.tensor.transpose(tp[:, u, a * P:(a + 1) * P], words[:, a, :, u], ident[:])
@@ -150,16 +144,13 @@ def tile_simplifiedretnet_pb_t_kernel(tc, h_ret, x, W1, b1, W2, b2, ln_g, ln_b, 
             nc.vector.quantize_mx(out=w2_codes[:].bitcast(FP8X4), scales=w2_scales[:], in_=t[:])
 
         def constants():
-            nc.tensor.matmul(out=ln_c[:, 0:D], lhsT=sixteens[:], rhs=rows[:, D:2 * D],
+            nc.tensor.matmul(out=ln_b_bank[:, 0:D], lhsT=ones[:], rhs=rows[:, D:2 * D],
                              start=True, stop=True)
-            nc.tensor.matmul(out=ln_c[:, D:2 * D], lhsT=ones[:], rhs=rows[:, 2 * D:3 * D],
-                             start=True, stop=True)
-            o = psum_o.tile([P, 2, D], F32, name="o")
-            nc.tensor.matmul(out=o[:, 0, :], lhsT=ones[:], rhs=rows[:, 0:D], start=True, stop=True)
-            nc.vector.tensor_copy(out=b2_b[:], in_=o[:, 0, :])
+            g_bank = psum_y.tile([P, 2, D], F32, name="y")
+            nc.tensor.matmul(out=g_bank[:, 0, :], lhsT=ones[:], rhs=rows[:, 0:D], start=True, stop=True)
+            nc.vector.tensor_copy(out=ln_g_b[:], in_=g_bank[:, 0, :])
 
-        def first_pass(n):
-            g, c = n // TILES, n % TILES
+        def first_pass(g, c):
             z = psum_z.tile([P, GROUP], F32, name="z")
             nc.tensor.matmul_mx(
                 out=z[:],
@@ -169,30 +160,37 @@ def tile_simplifiedretnet_pb_t_kernel(tc, h_ret, x, W1, b1, W2, b2, ln_g, ln_b, 
                 rhs_scale=codes[g][1][:],
                 start=True, stop=True,
             )
-            z_banks[n] = z
+            z_banks[(g, c)] = z
 
-        def gelu(g):
-            planes[g] = two.tile([P, TILES, GROUP], BF16, name="planes")
-            for c in range(TILES):
-                n = TILES * g + c
-                nc.scalar.activation(out=planes[g][:, c, :], in_=z_banks[n][:], func=ACT.Gelu,
-                                     bias=b1_c[:, c:c + 1], scale=1.0)
-                if n + Z_BANKS < TILES * N_GROUPS:
-                    first_pass(n + Z_BANKS)
+        def gelu(g, c):
+            if c == 0:
+                planes[g] = two.tile([P, TILES, GROUP], BF16, name="planes")
+            nc.scalar.activation(out=planes[g][:, c, :], in_=z_banks[(g, c)][:], func=ACT.Gelu,
+                                 bias=b1_c[:, c:c + 1], scale=1.0)
+            ahead_g, ahead_c = (g, c + 2) if c < 2 else (g + 1, c - 2)
+            if ahead_g < N_GROUPS:
+                first_pass(ahead_g, ahead_c)
+
+        def regrouped(g):
+            g_grouped[g] = three.tile([P, GROUP, 4], BF16, name="g_grouped", align_bytes=64)
+
+        def regroup_on_pool(g):
+            nc.gpsimd.tensor_scalar(
+                out=g_grouped[g][:, :POOL_TOKENS, :],
+                in0=planes[g][:, :, :POOL_TOKENS].rearrange("p t w -> p w t"),
+                scalar1=1.0, scalar2=0.0, op0=ALU.mult, op1=ALU.add)
 
         def regroup_on_scalar(g):
-            g_grouped[g] = three.tile([P, GROUP, 4], BF16, name="g_grouped", align_bytes=64)
-            cut = GROUP - SCALAR_TOKENS
+            lo, hi = POOL_TOKENS, POOL_TOKENS + SCALAR_TOKENS
             nc.scalar.copy(
-                out=g_grouped[g][:, cut:, :].rearrange("p (c i) t -> p c t i", i=4),
-                in_=planes[g][:, :, cut:].rearrange("p t (c i) -> p c t i", i=4),
+                out=g_grouped[g][:, lo:hi, :].rearrange("p (c i) t -> p c t i", i=4),
+                in_=planes[g][:, :, lo:hi].rearrange("p t (c i) -> p c t i", i=4),
             )
 
-        def regroup(g):
-            cut = GROUP - SCALAR_TOKENS
+        def regroup(g, lo):
             nc.vector.tensor_copy(
-                out=g_grouped[g][:, :cut, :].rearrange("p (c i) t -> p c t i", i=4),
-                in_=planes[g][:, :, :cut].rearrange("p t (c i) -> p c t i", i=4),
+                out=g_grouped[g][:, lo:, :].rearrange("p (c i) t -> p c t i", i=4),
+                in_=planes[g][:, :, lo:].rearrange("p t (c i) -> p c t i", i=4),
             )
 
         def quantise_g(g):
@@ -201,119 +199,149 @@ def tile_simplifiedretnet_pb_t_kernel(tc, h_ret, x, W1, b1, W2, b2, ln_g, ln_b, 
             nc.vector.quantize_mx(out=g_codes[g][0][:].bitcast(FP8X4), scales=g_codes[g][1][:],
                                   in_=g_grouped[g][:].rearrange("p w j -> p (w j)"))
 
-        def add_bias(g):
-            for j in range(POOL_TILES):
-                xb[(g, j)] = xb_pool.tile([P, D], F32, name="xb")
-                nc.gpsimd.tensor_tensor(out=xb[(g, j)][:], in0=x_sb[g][:, j, :], in1=b2_b[:],
-                                        op=ALU.add)
+        def second_pass(g, a):
+            o = psum_o.tile([P, GROUP], F32, name="o")
+            nc.tensor.matmul_mx(
+                out=o[:],
+                lhsT=w2_codes[:, a * P:(a + 1) * P].bitcast(FP8X4),
+                lhsT_scale=w2_scales[:, a * P:(a + 1) * P],
+                rhs=g_codes[g][0][:].bitcast(FP8X4),
+                rhs_scale=g_codes[g][1][:],
+                start=True, stop=True,
+            )
+            o_banks[(g, a)] = o
 
-        def add_bias_on_vector(g):
-            for j in range(POOL_TILES, TILES):
-                xb[(g, j)] = xbv_pool.tile([P, D], F32, name="xbv")
-                nc.vector.tensor_tensor(out=xb[(g, j)][:], in0=x_sb[g][:, j, :], in1=b2_b[:],
-                                        op=ALU.add)
-
-        def second_matmul(g):
-            for b in range(2):
-                o = psum_o.tile([P, 2, D], F32, name="o")
-                for jj in range(2):
-                    j = 2 * b + jj
-                    nc.tensor.matmul_mx(
-                        out=o[:, jj, :],
-                        lhsT=g_codes[g][0][:, j * P:(j + 1) * P].bitcast(FP8X4),
-                        lhsT_scale=g_codes[g][1][:, j * P:(j + 1) * P],
-                        rhs=w2_codes[:].bitcast(FP8X4),
-                        rhs_scale=w2_scales[:],
-                        start=True, stop=True,
-                    )
-                o_banks[(g, b)] = o
+        def evacuate(g, a):
+            if a == 0:
+                o_t[g] = two.tile([P, 2, GROUP], F32, name="o_t")
+            nc.scalar.activation(out=o_t[g][:, a, :], in_=o_banks[(g, a)][:], func=ACT.Identity,
+                                 bias=b2_c[:, a:a + 1], scale=1.0)
 
         def residual(g):
-            y[g] = three.tile([P, TILES, D], F32, name="y")
-            stats[g] = (four.tile([P, TILES], F32, name="sums"),
-                        four.tile([P, TILES], F32, name="negmu"),
-                        four.tile([P, TILES], F32, name="ssq"),
-                        four.tile([P, TILES], F32, name="rstd"))
-            for j in range(TILES):
-                nc.vector.scalar_tensor_tensor(
-                    out=y[g][:, j, :], in0=o_banks[(g, j // 2)][:, j % 2, :], scalar=0.0,
-                    in1=xb[(g, j)][:], op0=ALU.add, op1=ALU.add,
-                    accum_out=stats[g][0][:, j:j + 1],
-                )
+            for b in range(2):
+                y = psum_y.tile([P, 2, D], F32, name="y")
+                for jj in range(2):
+                    j = 2 * b + jj
+                    nc.tensor.matmul(out=y[:, jj, :], lhsT=ident_b[:], rhs=x_sb[g][:, j, :],
+                                     start=True, stop=False)
+                    for a in range(2):
+                        nc.tensor.matmul(out=y[:, jj, a * P:(a + 1) * P],
+                                         lhsT=o_t[g][:, a, j * P:(j + 1) * P], rhs=ident[:],
+                                         is_transpose=True, start=False, stop=(a == 1))
+                y_banks[(g, b)] = y
 
-        def variance(g):
-            nc.scalar.mul(out=stats[g][1][:], in_=stats[g][0][:], mul=-1.0 / D)
-            for j in range(TILES):
-                junk = two.tile([P, D], BF16, name="junk")
-                nc.scalar.activation(out=junk[:], in_=y[g][:, j, :], func=ACT.Square,
-                                     bias=stats[g][1][:, j:j + 1], scale=1.0,
-                                     accum_out=stats[g][2][:, j:j + 1])
+        def statistics(g):
+            moments[g] = (four.tile([P, TILES, 6], F32, name="halves"),
+                          four.tile([P, TILES, 2], F32, name="mean_var"),
+                          four.tile([P, TILES], F32, name="var_eps"),
+                          four.tile([P, TILES], F32, name="rstd"))
+            for b in range(2):
+                for jj in range(2):
+                    nc.vector.bn_stats(out=moments[g][0][:, 2 * b + jj, :],
+                                       in_=y_banks[(g, b)][:, jj, :])
+                for jj in range(2):
+                    nc.vector.bn_aggr(out=moments[g][1][:, 2 * b + jj, :],
+                                      in_=moments[g][0][:, 2 * b + jj, :])
 
         def add_eps(g):
-            nc.vector.tensor_scalar_add(out=stats[g][2][:], in0=stats[g][2][:],
-                                        scalar1=D * LN_EPS)
+            nc.vector.tensor_scalar_add(out=moments[g][2][:], in0=moments[g][1][:, :, 1],
+                                        scalar1=LN_EPS)
 
         def inverse_deviation(g):
-            nc.gpsimd.tensor_tensor(out=stats[g][3][:], in0=stats[g][2][:], in1=minus_half[:],
+            nc.gpsimd.tensor_tensor(out=moments[g][3][:], in0=moments[g][2][:], in1=minus_half[:],
                                     op=ALU.pow)
 
         def centre_and_gain(g):
             res[g] = four.tile([P, TILES, D], F32, name="res")
             for j in range(TILES):
                 nc.vector.scalar_tensor_tensor(
-                    out=res[g][:, j, :], in0=y[g][:, j, :], scalar=stats[g][1][:, j:j + 1],
-                    in1=ln_c[:, 0:D], op0=ALU.add, op1=ALU.mult,
+                    out=res[g][:, j, :], in0=y_banks[(g, j // 2)][:, j % 2, :],
+                    scalar=moments[g][1][:, j, 0:1],
+                    in1=ln_g_b[:], op0=ALU.subtract, op1=ALU.mult,
                 )
 
         def scale_and_shift(g):
             for j in range(TILES):
                 nc.vector.scalar_tensor_tensor(
-                    out=res[g][:, j, :], in0=res[g][:, j, :], scalar=stats[g][3][:, j:j + 1],
-                    in1=ln_c[:, D:2 * D], op0=ALU.mult, op1=ALU.add,
+                    out=res[g][:, j, :], in0=res[g][:, j, :], scalar=moments[g][3][:, j:j + 1],
+                    in1=ln_b_bank[:, 0:D], op0=ALU.mult, op1=ALU.add,
                 )
                 if g == N_GROUPS - 1:
                     nc.sync.dma_start(out=out_view[g][:, j, :], in_=res[g][:, j, :])
             if g < N_GROUPS - 1:
                 nc.sync.dma_start(out=out_view[g], in_=res[g][:])
 
-        def run(stage, g, first=0):
-            if first <= g < N_GROUPS:
-                stage(g)
+        def have(g):
+            return 0 <= g < N_GROUPS
 
         transposes("w")
-        copies("w", ("scalar", "vector"))
+        copy_half("w", 0)
+        copy_half("w", 1, "vector")
         quantise("w")
         transposes(0)
-        copies(0, ("scalar", "vector"))
+        copy_half(0, 0)
+        copy_half(0, 1, "vector")
         quantise(0)
         transposes(1)
-        for n in range(Z_BANKS):
-            first_pass(n)
-        copies(1)
+        first_pass(0, 0)
+        first_pass(0, 1)
+        copy_half(1, 0)
+        copy_half(1, 1)
+        second_weight()
         quantise(1)
         constants()
-        second_weight()
-        transposes(2)
-        add_bias(0)
-        add_bias_on_vector(0)
-        gelu(0)
-        copies(2)
-        transposes(3)
 
-        for i in range(-2, N_GROUPS + 1):
-            run(gelu, i + 2, 1)
-            run(copies, i + 5, 3)
-            run(transposes, i + 6, 4)
-            run(regroup_on_scalar, i + 2)
-            run(regroup, i + 1)
-            run(add_eps, i - 1)
-            run(quantise, i + 4, 2)
-            run(quantise_g, i + 1)
-            run(add_bias_on_vector, i + 2, 1)
-            run(second_matmul, i + 1)
-            run(residual, i)
-            run(variance, i)
-            run(inverse_deviation, i - 1)
-            run(add_bias, i + 2, 1)
-            run(scale_and_shift, i - 1)
-            run(centre_and_gain, i)
+        for i in range(N_GROUPS + 4):
+            early = i < EARLY_GROUPS
+            shared = EARLY_GROUPS <= i - 1 < N_GROUPS
+            if have(i):
+                gelu(i, 0)
+                gelu(i, 1)
+            if i == 0:
+                transposes(2)
+            if shared:
+                regroup(i - 1, POOL_TOKENS + SCALAR_TOKENS)
+            if have(i + 2) and not early:
+                quantise(i + 2)
+            if shared:
+                quantise_g(i - 1)
+            if have(i):
+                gelu(i, 2)
+            if have(i - 1):
+                second_pass(i - 1, 0)
+            if have(i):
+                gelu(i, 3)
+            if i == 0:
+                copy_half(2, 0)
+                copy_half(2, 1)
+            if have(i + 3):
+                transposes(i + 3)
+            if have(i - 3):
+                add_eps(i - 3)
+                inverse_deviation(i - 3)
+            if have(i):
+                regrouped(i)
+                if early:
+                    regroup(i, 0)
+                    quantise_g(i)
+                    quantise(i + 2)
+                else:
+                    regroup_on_pool(i)
+                    regroup_on_scalar(i)
+            if have(i - 2):
+                statistics(i - 2)
+            if have(i - 3):
+                scale_and_shift(i - 3)
+            if have(i - 2):
+                centre_and_gain(i - 2)
+            if have(i - 1):
+                evacuate(i - 1, 0)
+                second_pass(i - 1, 1)
+            if have(i + 3):
+                copy_half(i + 3, 0)
+            if have(i - 1):
+                evacuate(i - 1, 1)
+            if have(i + 3):
+                copy_half(i + 3, 1)
+            if have(i - 1):
+                residual(i - 1)

@@ -63,6 +63,9 @@ def tile_simplifiedretnet_pb_t_kernel(tc, h_ret, x, W1, b1, W2, b2, ln_g, ln_b, 
         with nc.allow_non_contiguous_dma("128 pieces of two bytes a half"):
             nc.scalar.dma_start(out=b2_c[:], in_=b2.rearrange("(a p) -> p a", p=P))
 
+        warm = keep.tile([P, 1], F32, name="warm")
+        nc.scalar.activation(out=warm[:], in_=minus_half[:, 0:1], func=ACT.Gelu)
+
         w1_sb = keep.tile([P, TILES, H], BF16, name="w1_sb")
         w2_sb = keep.tile([P, 2, F], BF16, name="w2_sb")
         src = {"w": w1_sb}
@@ -217,31 +220,54 @@ def tile_simplifiedretnet_pb_t_kernel(tc, h_ret, x, W1, b1, W2, b2, ln_g, ln_b, 
             nc.scalar.activation(out=o_t[g][:, a, :], in_=o_banks[(g, a)][:], func=ACT.Identity,
                                  bias=b2_c[:, a:a + 1], scale=1.0)
 
-        def residual(g):
+        def add_x(g):
             for b in range(2):
                 y = psum_y.tile([P, 2, D], F32, name="y")
-                for jj in range(2):
-                    j = 2 * b + jj
-                    nc.tensor.matmul(out=y[:, jj, :], lhsT=ident_b[:], rhs=x_sb[g][:, j, :],
-                                     start=True, stop=False)
-                    for a in range(2):
-                        nc.tensor.matmul(out=y[:, jj, a * P:(a + 1) * P],
-                                         lhsT=o_t[g][:, a, j * P:(j + 1) * P], rhs=ident[:],
-                                         is_transpose=True, start=False, stop=(a == 1))
+                nc.tensor.matmul(out=y[:], lhsT=ident_b[:], rhs=x_sb[g][:, 2 * b:2 * b + 2, :],
+                                 start=True, stop=False)
                 y_banks[(g, b)] = y
 
-        def statistics(g):
+        def add_product(g):
+            for b in range(2):
+                for jj in range(2):
+                    j = 2 * b + jj
+                    for a in range(2):
+                        nc.tensor.matmul(out=y_banks[(g, b)][:, jj, a * P:(a + 1) * P],
+                                         lhsT=o_t[g][:, a, j * P:(j + 1) * P], rhs=ident[:],
+                                         is_transpose=True, start=False,
+                                         stop=(jj == 1 and a == 1))
+
+        def moments_and_gain(g):
             moments[g] = (four.tile([P, TILES, 6], F32, name="halves"),
                           four.tile([P, TILES, 2], F32, name="mean_var"),
                           four.tile([P, TILES], F32, name="var_eps"),
                           four.tile([P, TILES], F32, name="rstd"))
-            for b in range(2):
-                for jj in range(2):
-                    nc.vector.bn_stats(out=moments[g][0][:, 2 * b + jj, :],
-                                       in_=y_banks[(g, b)][:, jj, :])
-                for jj in range(2):
-                    nc.vector.bn_aggr(out=moments[g][1][:, 2 * b + jj, :],
-                                      in_=moments[g][0][:, 2 * b + jj, :])
+            res[g] = four.tile([P, TILES, D], F32, name="res")
+            halves, mean_var = moments[g][0], moments[g][1]
+
+            def stats(j):
+                nc.vector.bn_stats(out=halves[:, j, :], in_=y_banks[(g, j // 2)][:, j % 2, :])
+
+            def aggregate(j):
+                nc.vector.bn_aggr(out=mean_var[:, j, :], in_=halves[:, j, :])
+
+            def gain(j):
+                nc.vector.scalar_tensor_tensor(
+                    out=res[g][:, j, :], in0=y_banks[(g, j // 2)][:, j % 2, :],
+                    scalar=mean_var[:, j, 0:1], in1=ln_g_b[:], op0=ALU.subtract, op1=ALU.mult)
+
+            stats(0)
+            stats(1)
+            aggregate(0)
+            stats(2)
+            aggregate(1)
+            stats(3)
+            aggregate(2)
+            gain(0)
+            aggregate(3)
+            gain(1)
+            gain(2)
+            gain(3)
 
         def add_eps(g):
             nc.vector.tensor_scalar_add(out=moments[g][2][:], in0=moments[g][1][:, :, 1],
@@ -250,15 +276,6 @@ def tile_simplifiedretnet_pb_t_kernel(tc, h_ret, x, W1, b1, W2, b2, ln_g, ln_b, 
         def inverse_deviation(g):
             nc.gpsimd.tensor_tensor(out=moments[g][3][:], in0=moments[g][2][:], in1=minus_half[:],
                                     op=ALU.pow)
-
-        def centre_and_gain(g):
-            res[g] = four.tile([P, TILES, D], F32, name="res")
-            for j in range(TILES):
-                nc.vector.scalar_tensor_tensor(
-                    out=res[g][:, j, :], in0=y_banks[(g, j // 2)][:, j % 2, :],
-                    scalar=moments[g][1][:, j, 0:1],
-                    in1=ln_g_b[:], op0=ALU.subtract, op1=ALU.mult,
-                )
 
         def scale_and_shift(g):
             for j in range(TILES):
@@ -274,6 +291,7 @@ def tile_simplifiedretnet_pb_t_kernel(tc, h_ret, x, W1, b1, W2, b2, ln_g, ln_b, 
         def have(g):
             return 0 <= g < N_GROUPS
 
+        constants()
         transposes("w")
         copy_half("w", 0)
         copy_half("w", 1, "vector")
@@ -283,65 +301,56 @@ def tile_simplifiedretnet_pb_t_kernel(tc, h_ret, x, W1, b1, W2, b2, ln_g, ln_b, 
         copy_half(0, 1, "vector")
         quantise(0)
         transposes(1)
+        second_weight()
         first_pass(0, 0)
         first_pass(0, 1)
         copy_half(1, 0)
         copy_half(1, 1)
-        second_weight()
         quantise(1)
-        constants()
+        transposes(2)
 
-        for i in range(N_GROUPS + 4):
+        for i in range(N_GROUPS + 3):
             early = i < EARLY_GROUPS
-            shared = EARLY_GROUPS <= i - 1 < N_GROUPS
             if have(i):
                 gelu(i, 0)
                 gelu(i, 1)
-            if i == 0:
-                transposes(2)
-            if shared:
-                regroup(i - 1, POOL_TOKENS + SCALAR_TOKENS)
-            if have(i + 2) and not early:
-                quantise(i + 2)
-            if shared:
-                quantise_g(i - 1)
+            if have(i + 2):
+                copy_half(i + 2, 0)
+            if have(i - 2):
+                moments_and_gain(i - 2)
             if have(i):
                 gelu(i, 2)
             if have(i - 1):
                 second_pass(i - 1, 0)
             if have(i):
                 gelu(i, 3)
-            if i == 0:
-                copy_half(2, 0)
-                copy_half(2, 1)
+            if have(i - 1):
+                evacuate(i - 1, 0)
+                second_pass(i - 1, 1)
+                add_x(i - 1)
+            if have(i + 2):
+                copy_half(i + 2, 1)
             if have(i + 3):
                 transposes(i + 3)
-            if have(i - 3):
-                add_eps(i - 3)
-                inverse_deviation(i - 3)
             if have(i):
                 regrouped(i)
                 if early:
                     regroup(i, 0)
                     quantise_g(i)
-                    quantise(i + 2)
                 else:
                     regroup_on_pool(i)
                     regroup_on_scalar(i)
-            if have(i - 2):
-                statistics(i - 2)
-            if have(i - 3):
-                scale_and_shift(i - 3)
-            if have(i - 2):
-                centre_and_gain(i - 2)
-            if have(i - 1):
-                evacuate(i - 1, 0)
-                second_pass(i - 1, 1)
-            if have(i + 3):
-                copy_half(i + 3, 0)
             if have(i - 1):
                 evacuate(i - 1, 1)
-            if have(i + 3):
-                copy_half(i + 3, 1)
-            if have(i - 1):
-                residual(i - 1)
+                add_product(i - 1)
+            if have(i - 3):
+                scale_and_shift(i - 3)
+            if have(i) and not early:
+                regroup(i, POOL_TOKENS + SCALAR_TOKENS)
+            if have(i + 2):
+                quantise(i + 2)
+            if have(i) and not early:
+                quantise_g(i)
+            if have(i - 2):
+                add_eps(i - 2)
+                inverse_deviation(i - 2)

@@ -23,6 +23,7 @@ LN_EPS = 1e-5
 POOL_TOKENS = 320
 SCALAR_TOKENS = 64
 EARLY_GROUPS = 2
+LATE_GROUPS = 2
 
 FLOPS = 2 * TOKENS * H * F + 2 * TOKENS * F * D
 
@@ -73,8 +74,11 @@ def tile_simplifiedretnet_pb_t_kernel(tc, h_ret, x, W1, b1, W2, b2, ln_g, ln_b, 
         for g in range(N_GROUPS):
             src[g] = keep.tile([P, TILES, H], BF16, name="h%d" % g)
             x_sb[g] = keep.tile([P, TILES, D], BF16, name="x%d" % g)
-        nc.sync.dma_start(out=w1_sb[:], in_=W1.rearrange("(m c) k -> m c k", c=TILES))
-        nc.sync.dma_start(out=src[0][:], in_=h_view[0])
+        w1_view = W1.rearrange("(m c) k -> m c k", c=TILES)
+        for b in range(2):
+            nc.sync.dma_start(out=src[0][:, 2 * b:2 * b + 2, :], in_=h_view[0][:, 2 * b:2 * b + 2, :])
+        for b in range(2):
+            nc.sync.dma_start(out=w1_sb[:, 2 * b:2 * b + 2, :], in_=w1_view[:, 2 * b:2 * b + 2, :])
         nc.sync.dma_start(out=src[1][:], in_=h_view[1])
         nc.sync.dma_start(out=w2_sb[:], in_=W2.rearrange("(a p) f -> p a f", p=P))
         nc.sync.dma_start(out=src[2][:], in_=h_view[2])
@@ -93,7 +97,7 @@ def tile_simplifiedretnet_pb_t_kernel(tc, h_ret, x, W1, b1, W2, b2, ln_g, ln_b, 
 
         banks = {}
         grouped = {}
-        codes = {"w": (w1_codes, w1_scales)}
+        codes = {}
         planes = {}
         z_banks = {}
         g_grouped = {}
@@ -104,10 +108,13 @@ def tile_simplifiedretnet_pb_t_kernel(tc, h_ret, x, W1, b1, W2, b2, ln_g, ln_b, 
         moments = {}
         res = {}
 
-        def transposes(key, halves=(0, 1)):
+        def transposes(key):
             words = src[key][:].bitcast(F32)
-            for b in halves:
-                tp = psum_t.tile([P, 2, 2 * P], F32, name="tp")
+            for b in range(2):
+                if key == "w":
+                    tp = psum_y.tile([P, 2, 2 * P], F32, name="y")
+                else:
+                    tp = psum_t.tile([P, 2, 2 * P], F32, name="tp")
                 for jj in range(2):
                     for u in range(2):
                         nc.tensor.transpose(
@@ -128,12 +135,16 @@ def tile_simplifiedretnet_pb_t_kernel(tc, h_ret, x, W1, b1, W2, b2, ln_g, ln_b, 
             else:
                 nc.scalar.copy(out=dst, in_=source)
 
-        def quantise(key):
-            if key != "w":
-                codes[key] = (four.tile([P, GROUP], U32, name="h_codes", align_bytes=64),
-                              four.tile([P, GROUP], U8, name="h_scales", align_bytes=64))
-            nc.vector.quantize_mx(out=codes[key][0][:].bitcast(FP8X4), scales=codes[key][1][:],
-                                  in_=grouped[key][:])
+        def quantise(g):
+            codes[g] = (four.tile([P, GROUP], U32, name="h_codes", align_bytes=64),
+                        four.tile([P, GROUP], U8, name="h_scales", align_bytes=64))
+            nc.vector.quantize_mx(out=codes[g][0][:].bitcast(FP8X4), scales=codes[g][1][:],
+                                  in_=grouped[g][:])
+
+        def quantise_first_weight(b):
+            cols = slice(b * 2 * P, (b + 1) * 2 * P)
+            nc.vector.quantize_mx(out=w1_codes[:, cols].bitcast(FP8X4), scales=w1_scales[:, cols],
+                                  in_=grouped["w"][:, b * 8 * P:(b + 1) * 8 * P])
 
         def second_weight():
             words = w2_sb[:].bitcast(F32).rearrange("p a (q u) -> p a q u", u=2)
@@ -183,8 +194,8 @@ def tile_simplifiedretnet_pb_t_kernel(tc, h_ret, x, W1, b1, W2, b2, ln_g, ln_b, 
                 in0=planes[g][:, :, :POOL_TOKENS].rearrange("p t w -> p w t"),
                 scalar1=1.0, scalar2=0.0, op0=ALU.mult, op1=ALU.add)
 
-        def regroup_on_scalar(g):
-            lo, hi = POOL_TOKENS, POOL_TOKENS + SCALAR_TOKENS
+        def regroup_on_scalar(g, hi):
+            lo = POOL_TOKENS
             nc.scalar.copy(
                 out=g_grouped[g][:, lo:hi, :].rearrange("p (c i) t -> p c t i", i=4),
                 in_=planes[g][:, :, lo:hi].rearrange("p t (c i) -> p c t i", i=4),
@@ -266,6 +277,9 @@ def tile_simplifiedretnet_pb_t_kernel(tc, h_ret, x, W1, b1, W2, b2, ln_g, ln_b, 
             gain(0)
             aggregate(3)
             gain(1)
+            if g == N_GROUPS - 1:
+                add_eps(g)
+                inverse_deviation(g)
             gain(2)
             gain(3)
 
@@ -291,46 +305,48 @@ def tile_simplifiedretnet_pb_t_kernel(tc, h_ret, x, W1, b1, W2, b2, ln_g, ln_b, 
         def have(g):
             return 0 <= g < N_GROUPS
 
-        constants()
-        transposes("w")
-        copy_half("w", 0)
-        copy_half("w", 1, "vector")
-        quantise("w")
         transposes(0)
+        transposes("w")
         copy_half(0, 0)
         copy_half(0, 1, "vector")
+        copy_half("w", 0)
+        copy_half("w", 1)
         quantise(0)
-        transposes(1)
-        second_weight()
+        quantise_first_weight(0)
+        quantise_first_weight(1)
         first_pass(0, 0)
         first_pass(0, 1)
-        copy_half(1, 0)
-        copy_half(1, 1)
+        transposes(1)
+        copy_half(1, 0, "vector")
+        copy_half(1, 1, "vector")
         quantise(1)
-        transposes(2)
 
         for i in range(N_GROUPS + 3):
             early = i < EARLY_GROUPS
+            late = i >= N_GROUPS - LATE_GROUPS
             if have(i):
                 gelu(i, 0)
                 gelu(i, 1)
-            if have(i + 2):
+            if i == 0:
+                second_weight()
+                constants()
+                transposes(2)
+            if have(i + 2) and not early:
                 copy_half(i + 2, 0)
             if have(i - 2):
                 moments_and_gain(i - 2)
-            if have(i):
-                gelu(i, 2)
             if have(i - 1):
                 second_pass(i - 1, 0)
             if have(i):
+                gelu(i, 2)
                 gelu(i, 3)
             if have(i - 1):
                 evacuate(i - 1, 0)
                 second_pass(i - 1, 1)
                 add_x(i - 1)
             if have(i + 2):
-                copy_half(i + 2, 1)
-            if have(i + 3):
+                copy_half(i + 2, 0 if early else 1)
+            if have(i + 3) and not early:
                 transposes(i + 3)
             if have(i):
                 regrouped(i)
@@ -339,18 +355,21 @@ def tile_simplifiedretnet_pb_t_kernel(tc, h_ret, x, W1, b1, W2, b2, ln_g, ln_b, 
                     quantise_g(i)
                 else:
                     regroup_on_pool(i)
-                    regroup_on_scalar(i)
+                    regroup_on_scalar(i, GROUP if late else POOL_TOKENS + SCALAR_TOKENS)
             if have(i - 1):
                 evacuate(i - 1, 1)
                 add_product(i - 1)
+            if early:
+                copy_half(i + 2, 1)
+                transposes(i + 3)
             if have(i - 3):
                 scale_and_shift(i - 3)
-            if have(i) and not early:
+            if have(i) and not early and not late:
                 regroup(i, POOL_TOKENS + SCALAR_TOKENS)
             if have(i + 2):
                 quantise(i + 2)
             if have(i) and not early:
                 quantise_g(i)
-            if have(i - 2):
+            if have(i - 2) and i - 2 < N_GROUPS - 1:
                 add_eps(i - 2)
                 inverse_deviation(i - 2)

@@ -52,6 +52,8 @@ def tile_simplifiedretnet_pb_t_kernel(tc, h_ret, x, W1, b1, W2, b2, ln_g, ln_b, 
         nc.vector.memset(rows[:], 0.0)
         ones = keep.tile([P, P], BF16, name="ones")
         nc.vector.memset(ones[:], 1.0)
+        sixteens = keep.tile([P, P], BF16, name="sixteens")
+        nc.vector.memset(sixteens[:], 16.0)
         minus_half = keep.tile([P, TILES], F32, name="minus_half")
         nc.vector.memset(minus_half[:], -0.5)
         ident_b = keep.tile([P, P], BF16, name="ident_b")
@@ -161,7 +163,7 @@ def tile_simplifiedretnet_pb_t_kernel(tc, h_ret, x, W1, b1, W2, b2, ln_g, ln_b, 
             nc.tensor.matmul(out=ln_b_bank[:, 0:D], lhsT=ones[:], rhs=rows[:, D:2 * D],
                              start=True, stop=True)
             g_bank = psum_y.tile([P, 2, D], F32, name="y")
-            nc.tensor.matmul(out=g_bank[:, 0, :], lhsT=ones[:], rhs=rows[:, 0:D], start=True, stop=True)
+            nc.tensor.matmul(out=g_bank[:, 0, :], lhsT=sixteens[:], rhs=rows[:, 0:D], start=True, stop=True)
             nc.vector.tensor_copy(out=ln_g_b[:], in_=g_bank[:, 0, :])
 
         def first_pass(g, c):
@@ -249,52 +251,33 @@ def tile_simplifiedretnet_pb_t_kernel(tc, h_ret, x, W1, b1, W2, b2, ln_g, ln_b, 
                                          stop=(jj == 1 and a == 1))
 
         def moments_and_gain(g):
-            moments[g] = (four.tile([P, TILES, 6], F32, name="halves"),
-                          four.tile([P, TILES, 2], F32, name="mean_var"),
-                          four.tile([P, TILES], F32, name="var_eps"),
+            moments[g] = (four.tile([P, TILES, 3], F32, name="moments"),
+                          four.tile([P, TILES], F32, name="sum_eps"),
                           four.tile([P, TILES], F32, name="rstd"))
             res[g] = four.tile([P, TILES, D], F32, name="res")
-            halves, mean_var = moments[g][0], moments[g][1]
-
-            def stats(j):
-                nc.vector.bn_stats(out=halves[:, j, :], in_=y_banks[(g, j // 2)][:, j % 2, :])
-
-            def aggregate(j):
-                nc.vector.bn_aggr(out=mean_var[:, j, :], in_=halves[:, j, :])
-
-            def gain(j):
+            for b in range(2):
+                nc.vector.bn_stats(out=moments[g][0][:, 2 * b:2 * b + 2, :].rearrange("p j s -> p (j s)"),
+                                   in_=y_banks[(g, b)][:].rearrange("p j d -> p d j"))
+            for j in range(TILES):
                 nc.vector.scalar_tensor_tensor(
                     out=res[g][:, j, :], in0=y_banks[(g, j // 2)][:, j % 2, :],
-                    scalar=mean_var[:, j, 0:1], in1=ln_g_b[:], op0=ALU.subtract, op1=ALU.mult)
-
-            stats(0)
-            stats(1)
-            aggregate(0)
-            stats(2)
-            aggregate(1)
-            stats(3)
-            aggregate(2)
-            gain(0)
-            aggregate(3)
-            gain(1)
-            if g == N_GROUPS - 1:
-                add_eps(g)
-                inverse_deviation(g)
-            gain(2)
-            gain(3)
+                    scalar=moments[g][0][:, j, 1:2], in1=ln_g_b[:], op0=ALU.subtract, op1=ALU.mult)
+                if j == 1 and g == N_GROUPS - 1:
+                    add_eps(g)
+                    inverse_deviation(g)
 
         def add_eps(g):
-            nc.vector.tensor_scalar_add(out=moments[g][2][:], in0=moments[g][1][:, :, 1],
-                                        scalar1=LN_EPS)
+            nc.vector.tensor_scalar_add(out=moments[g][1][:], in0=moments[g][0][:, :, 2],
+                                        scalar1=D * LN_EPS)
 
         def inverse_deviation(g):
-            nc.gpsimd.tensor_tensor(out=moments[g][3][:], in0=moments[g][2][:], in1=minus_half[:],
+            nc.gpsimd.tensor_tensor(out=moments[g][2][:], in0=moments[g][1][:], in1=minus_half[:],
                                     op=ALU.pow)
 
         def scale_and_shift(g):
             for j in range(TILES):
                 nc.vector.scalar_tensor_tensor(
-                    out=res[g][:, j, :], in0=res[g][:, j, :], scalar=moments[g][3][:, j:j + 1],
+                    out=res[g][:, j, :], in0=res[g][:, j, :], scalar=moments[g][2][:, j:j + 1],
                     in1=ln_b_bank[:, 0:D], op0=ALU.mult, op1=ALU.add,
                 )
                 if g == N_GROUPS - 1:

@@ -20,7 +20,7 @@ GROUP = 512
 TILES = GROUP // P
 N_GROUPS = TOKENS // GROUP
 LN_EPS = 1e-5
-POOL_TOKENS = 320
+POOL_TOKENS = 384
 SCALAR_TOKENS = 64
 EARLY_GROUPS = 2
 LATE_GROUPS = 2
@@ -81,8 +81,8 @@ def tile_simplifiedretnet_pb_t_kernel(tc, h_ret, x, W1, b1, W2, b2, ln_g, ln_b, 
             nc.sync.dma_start(out=src[0][:, 2 * b:2 * b + 2, :], in_=h_view[0][:, 2 * b:2 * b + 2, :])
         for b in range(2):
             nc.sync.dma_start(out=w1_sb[:, 2 * b:2 * b + 2, :], in_=w1_view[:, 2 * b:2 * b + 2, :])
-        nc.sync.dma_start(out=src[1][:], in_=h_view[1])
         nc.sync.dma_start(out=w2_sb[:], in_=W2.rearrange("(a p) f -> p a f", p=P))
+        nc.sync.dma_start(out=src[1][:], in_=h_view[1])
         nc.sync.dma_start(out=src[2][:], in_=h_view[2])
         nc.sync.dma_start(out=src[3][:], in_=h_view[3])
         for g in range(N_GROUPS):
@@ -162,9 +162,10 @@ def tile_simplifiedretnet_pb_t_kernel(tc, h_ret, x, W1, b1, W2, b2, ln_g, ln_b, 
         def constants():
             nc.tensor.matmul(out=ln_b_bank[:, 0:D], lhsT=ones[:], rhs=rows[:, D:2 * D],
                              start=True, stop=True)
-            g_bank = psum_y.tile([P, 2, D], F32, name="y")
-            nc.tensor.matmul(out=g_bank[:, 0, :], lhsT=sixteens[:], rhs=rows[:, 0:D], start=True, stop=True)
-            nc.vector.tensor_copy(out=ln_g_b[:], in_=g_bank[:, 0, :])
+            bank = psum_o.tile([P, GROUP], F32, name="o")
+            nc.tensor.matmul(out=bank[:, 0:D], lhsT=sixteens[:], rhs=rows[:, 0:D],
+                             start=True, stop=True)
+            nc.scalar.copy(out=ln_g_b[:], in_=bank[:, 0:D])
 
         def first_pass(g, c):
             z = psum_z.tile([P, GROUP], F32, name="z")
@@ -267,8 +268,8 @@ def tile_simplifiedretnet_pb_t_kernel(tc, h_ret, x, W1, b1, W2, b2, ln_g, ln_b, 
                     inverse_deviation(g)
 
         def add_eps(g):
-            nc.vector.tensor_scalar_add(out=moments[g][1][:], in0=moments[g][0][:, :, 2],
-                                        scalar1=D * LN_EPS)
+            nc.gpsimd.tensor_scalar(out=moments[g][1][:], in0=moments[g][0][:, :, 2],
+                                    scalar1=1.0, scalar2=D * LN_EPS, op0=ALU.mult, op1=ALU.add)
 
         def inverse_deviation(g):
             nc.gpsimd.tensor_tensor(out=moments[g][2][:], in0=moments[g][1][:], in1=minus_half[:],
@@ -297,6 +298,8 @@ def tile_simplifiedretnet_pb_t_kernel(tc, h_ret, x, W1, b1, W2, b2, ln_g, ln_b, 
         quantise(0)
         quantise_first_weight(0)
         quantise_first_weight(1)
+        second_weight()
+        constants()
         first_pass(0, 0)
         first_pass(0, 1)
         transposes(1)
@@ -311,8 +314,6 @@ def tile_simplifiedretnet_pb_t_kernel(tc, h_ret, x, W1, b1, W2, b2, ln_g, ln_b, 
                 gelu(i, 0)
                 gelu(i, 1)
             if i == 0:
-                second_weight()
-                constants()
                 transposes(2)
             if have(i + 2) and not early:
                 copy_half(i + 2, 0)

@@ -20,8 +20,8 @@ GROUP = 512
 TILES = GROUP // P
 N_GROUPS = TOKENS // GROUP
 LN_EPS = 1e-5
-POOL_TOKENS = 384
-SCALAR_TOKENS = 64
+POOL_TOKENS = 288
+SCALAR_TOKENS = 96
 EARLY_GROUPS = 2
 LATE_GROUPS = 2
 
@@ -217,7 +217,10 @@ def tile_simplifiedretnet_pb_t_kernel(tc, h_ret, x, W1, b1, W2, b2, ln_g, ln_b, 
                                   in_=g_grouped[g][:].rearrange("p w j -> p (w j)"))
 
         def second_pass(g, a):
-            o = psum_o.tile([P, GROUP], F32, name="o")
+            if g == N_GROUPS - 1 and a == 1:
+                o = psum_z.tile([P, GROUP], F32, name="z")
+            else:
+                o = psum_o.tile([P, GROUP], F32, name="o")
             nc.tensor.matmul_mx(
                 out=o[:],
                 lhsT=w2_codes[:, a * P:(a + 1) * P].bitcast(FP8X4),
@@ -241,15 +244,12 @@ def tile_simplifiedretnet_pb_t_kernel(tc, h_ret, x, W1, b1, W2, b2, ln_g, ln_b, 
                                  start=True, stop=False)
                 y_banks[(g, b)] = y
 
-        def add_product(g):
-            for b in range(2):
-                for jj in range(2):
-                    j = 2 * b + jj
-                    for a in range(2):
-                        nc.tensor.matmul(out=y_banks[(g, b)][:, jj, a * P:(a + 1) * P],
-                                         lhsT=o_t[g][:, a, j * P:(j + 1) * P], rhs=ident[:],
-                                         is_transpose=True, start=False,
-                                         stop=(jj == 1 and a == 1))
+        def add_product(g, a):
+            for j in range(TILES):
+                b, jj = j // 2, j % 2
+                nc.tensor.matmul(out=y_banks[(g, b)][:, jj, a * P:(a + 1) * P],
+                                 lhsT=o_t[g][:, a, j * P:(j + 1) * P], rhs=ident[:],
+                                 is_transpose=True, start=False, stop=(a == 1 and jj == 1))
 
         def moments_and_gain(g):
             moments[g] = (four.tile([P, TILES, 3], F32, name="moments"),
@@ -268,8 +268,8 @@ def tile_simplifiedretnet_pb_t_kernel(tc, h_ret, x, W1, b1, W2, b2, ln_g, ln_b, 
                     inverse_deviation(g)
 
         def add_eps(g):
-            nc.gpsimd.tensor_scalar(out=moments[g][1][:], in0=moments[g][0][:, :, 2],
-                                    scalar1=1.0, scalar2=D * LN_EPS, op0=ALU.mult, op1=ALU.add)
+            nc.vector.tensor_scalar_add(out=moments[g][1][:], in0=moments[g][0][:, :, 2],
+                                        scalar1=D * LN_EPS)
 
         def inverse_deviation(g):
             nc.gpsimd.tensor_tensor(out=moments[g][2][:], in0=moments[g][1][:], in1=minus_half[:],
@@ -332,6 +332,8 @@ def tile_simplifiedretnet_pb_t_kernel(tc, h_ret, x, W1, b1, W2, b2, ln_g, ln_b, 
                 copy_half(i + 2, 0 if early else 1)
             if have(i + 3) and not early:
                 transposes(i + 3)
+            if have(i - 1):
+                add_product(i - 1, 0)
             if have(i):
                 regrouped(i)
                 if early:
@@ -342,7 +344,7 @@ def tile_simplifiedretnet_pb_t_kernel(tc, h_ret, x, W1, b1, W2, b2, ln_g, ln_b, 
                     regroup_on_scalar(i, GROUP if late else POOL_TOKENS + SCALAR_TOKENS)
             if have(i - 1):
                 evacuate(i - 1, 1)
-                add_product(i - 1)
+                add_product(i - 1, 1)
             if early:
                 copy_half(i + 2, 1)
                 transposes(i + 3)

@@ -24,6 +24,7 @@ POOL_TOKENS = 288
 SCALAR_TOKENS = 96
 EARLY_GROUPS = 2
 LATE_GROUPS = 2
+VECTOR_COPIED = 4
 
 FLOPS = 2 * TOKENS * H * F + 2 * TOKENS * F * D
 
@@ -263,17 +264,17 @@ def tile_simplifiedretnet_pb_t_kernel(tc, h_ret, x, W1, b1, W2, b2, ln_g, ln_b, 
                 nc.vector.scalar_tensor_tensor(
                     out=res[g][:, j, :], in0=y_banks[(g, j // 2)][:, j % 2, :],
                     scalar=moments[g][0][:, j, 1:2], in1=ln_g_b[:], op0=ALU.subtract, op1=ALU.mult)
-                if j == 1 and g == N_GROUPS - 1:
-                    add_eps(g)
-                    inverse_deviation(g)
+                if j < 2 and g == N_GROUPS - 1:
+                    add_eps(g, 2 * j, 2 * j + 2)
+                    inverse_deviation(g, 2 * j, 2 * j + 2)
 
-        def add_eps(g):
-            nc.vector.tensor_scalar_add(out=moments[g][1][:], in0=moments[g][0][:, :, 2],
+        def add_eps(g, lo=0, hi=TILES):
+            nc.vector.tensor_scalar_add(out=moments[g][1][:, lo:hi], in0=moments[g][0][:, lo:hi, 2],
                                         scalar1=D * LN_EPS)
 
-        def inverse_deviation(g):
-            nc.gpsimd.tensor_tensor(out=moments[g][2][:], in0=moments[g][1][:], in1=minus_half[:],
-                                    op=ALU.pow)
+        def inverse_deviation(g, lo=0, hi=TILES):
+            nc.gpsimd.tensor_tensor(out=moments[g][2][:, lo:hi], in0=moments[g][1][:, lo:hi],
+                                    in1=minus_half[:, lo:hi], op=ALU.pow)
 
         def scale_and_shift(g):
             for j in range(TILES):
@@ -315,8 +316,9 @@ def tile_simplifiedretnet_pb_t_kernel(tc, h_ret, x, W1, b1, W2, b2, ln_g, ln_b, 
                 gelu(i, 1)
             if i == 0:
                 transposes(2)
+            engine = "vector" if i + 2 == VECTOR_COPIED else "scalar"
             if have(i + 2) and not early:
-                copy_half(i + 2, 0)
+                copy_half(i + 2, 0, engine)
             if have(i - 2):
                 moments_and_gain(i - 2)
             if have(i - 1):
@@ -329,7 +331,7 @@ def tile_simplifiedretnet_pb_t_kernel(tc, h_ret, x, W1, b1, W2, b2, ln_g, ln_b, 
                 second_pass(i - 1, 1)
                 add_x(i - 1)
             if have(i + 2):
-                copy_half(i + 2, 0 if early else 1)
+                copy_half(i + 2, 0 if early else 1, engine)
             if have(i + 3) and not early:
                 transposes(i + 3)
             if have(i - 1):

@@ -20,11 +20,10 @@ GROUP = 512
 TILES = GROUP // P
 N_GROUPS = TOKENS // GROUP
 LN_EPS = 1e-5
-POOL_TOKENS = 288
+POOL_TOKENS = 320
 SCALAR_TOKENS = 96
 EARLY_GROUPS = 2
 LATE_GROUPS = 2
-VECTOR_COPIED = 4
 
 FLOPS = 2 * TOKENS * H * F + 2 * TOKENS * F * D
 
@@ -316,9 +315,8 @@ def tile_simplifiedretnet_pb_t_kernel(tc, h_ret, x, W1, b1, W2, b2, ln_g, ln_b, 
                 gelu(i, 1)
             if i == 0:
                 transposes(2)
-            engine = "vector" if i + 2 == VECTOR_COPIED else "scalar"
             if have(i + 2) and not early:
-                copy_half(i + 2, 0, engine)
+                copy_half(i + 2, 0)
             if have(i - 2):
                 moments_and_gain(i - 2)
             if have(i - 1):
@@ -331,7 +329,7 @@ def tile_simplifiedretnet_pb_t_kernel(tc, h_ret, x, W1, b1, W2, b2, ln_g, ln_b, 
                 second_pass(i - 1, 1)
                 add_x(i - 1)
             if have(i + 2):
-                copy_half(i + 2, 0 if early else 1, engine)
+                copy_half(i + 2, 0 if early else 1)
             if have(i + 3) and not early:
                 transposes(i + 3)
             if have(i - 1):

from contextlib import ExitStack

import concourse.mybir as mybir
from concourse.masks import make_identity

F32 = mybir.dt.float32
BF16 = mybir.dt.bfloat16
U32 = mybir.dt.uint32
U8 = mybir.dt.uint8
FP8X4 = mybir.dt.float8_e4m3fn_x4
ALU = mybir.AluOpType
ACT = mybir.ActivationFunctionType

P = 128
TOKENS = 4 * 2048
H = 512
F = 512
D = 256
GROUP = 512
TILES = GROUP // P
N_GROUPS = TOKENS // GROUP
LN_EPS = 1e-5
POOL_TOKENS = 320
SCALAR_TOKENS = 96
EARLY_GROUPS = 2
LATE_GROUPS = 2

FLOPS = 2 * TOKENS * H * F + 2 * TOKENS * F * D


def tile_simplifiedretnet_pb_t_kernel(tc, h_ret, x, W1, b1, W2, b2, ln_g, ln_b, out):
    nc = tc.nc
    h_view = h_ret.flatten_outer_dims().rearrange("(g p j) k -> g p j k", p=P, j=TILES)
    x_view = x.flatten_outer_dims().rearrange("(g p j) d -> g p j d", p=P, j=TILES)
    out_view = out.flatten_outer_dims().rearrange("(g p j) d -> g p j d", p=P, j=TILES)

    with ExitStack() as ctx:
        keep = ctx.enter_context(tc.tile_pool(name="keep", bufs=1))
        two = ctx.enter_context(tc.tile_pool(name="two", bufs=2))
        three = ctx.enter_context(tc.tile_pool(name="three", bufs=3))
        four = ctx.enter_context(tc.tile_pool(name="four", bufs=4))
        psum_t = ctx.enter_context(tc.psum_pool(name="psum_t", bufs=2))
        psum_z = ctx.enter_context(tc.psum_pool(name="psum_z", bufs=2))
        psum_o = ctx.enter_context(tc.psum_pool(name="psum_o", bufs=1))
        psum_y = ctx.enter_context(tc.psum_pool(name="psum_y", bufs=2))
        psum_c = ctx.enter_context(tc.psum_pool(name="psum_c", bufs=1))
        ctx.enter_context(tc.manual_schedule())

        ident = keep.tile([P, P], F32, name="ident")
        make_identity(nc, ident[:])
        rows = keep.tile([P, 2 * D], BF16, name="rows")
        nc.vector.memset(rows[:], 0.0)
        ones = keep.tile([P, P], BF16, name="ones")
        nc.vector.memset(ones[:], 1.0)
        sixteens = keep.tile([P, P], BF16, name="sixteens")
        nc.vector.memset(sixteens[:], 16.0)
        minus_half = keep.tile([P, TILES], F32, name="minus_half")
        nc.vector.memset(minus_half[:], -0.5)
        ident_b = keep.tile([P, P], BF16, name="ident_b")
        nc.vector.tensor_copy(out=ident_b[:], in_=ident[:])
        b1_c = keep.tile([P, TILES], BF16, name="b1_c")
        b2_c = keep.tile([P, 2], BF16, name="b2_c")
        nc.scalar.dma_start(out=b1_c[:], in_=b1.rearrange("(m c) -> m c", c=TILES))
        nc.scalar.dma_start(out=rows[0:1, 0:D], in_=ln_g.rearrange("(o d) -> o d", o=1))
        nc.scalar.dma_start(out=rows[0:1, D:2 * D], in_=ln_b.rearrange("(o d) -> o d", o=1))
        with nc.allow_non_contiguous_dma("128 pieces of two bytes a half"):
            nc.scalar.dma_start(out=b2_c[:], in_=b2.rearrange("(a p) -> p a", p=P))

        warm = keep.tile([P, 1], F32, name="warm")
        nc.scalar.activation(out=warm[:], in_=minus_half[:, 0:1], func=ACT.Gelu)

        w1_sb = keep.tile([P, TILES, H], BF16, name="w1_sb")
        w2_sb = keep.tile([P, 2, F], BF16, name="w2_sb")
        src = {"w": w1_sb}
        x_sb = {}
        for g in range(N_GROUPS):
            src[g] = keep.tile([P, TILES, H], BF16, name="h%d" % g)
            x_sb[g] = keep.tile([P, TILES, D], BF16, name="x%d" % g)
        w1_view = W1.rearrange("(m c) k -> m c k", c=TILES)
        for b in range(2):
            nc.sync.dma_start(out=src[0][:, 2 * b:2 * b + 2, :], in_=h_view[0][:, 2 * b:2 * b + 2, :])
        for b in range(2):
            nc.sync.dma_start(out=w1_sb[:, 2 * b:2 * b + 2, :], in_=w1_view[:, 2 * b:2 * b + 2, :])
        nc.sync.dma_start(out=w2_sb[:], in_=W2.rearrange("(a p) f -> p a f", p=P))
        nc.sync.dma_start(out=src[1][:], in_=h_view[1])
        nc.sync.dma_start(out=src[2][:], in_=h_view[2])
        nc.sync.dma_start(out=src[3][:], in_=h_view[3])
        for g in range(N_GROUPS):
            nc.sync.dma_start(out=x_sb[g][:], in_=x_view[g])
            if g + 4 < N_GROUPS:
                nc.sync.dma_start(out=src[g + 4][:], in_=h_view[g + 4])

        w1_codes = keep.tile([P, F], U32, name="w1_codes", align_bytes=64)
        w1_scales = keep.tile([P, F], U8, name="w1_scales", align_bytes=64)
        w2_codes = keep.tile([P, D], U32, name="w2_codes", align_bytes=64)
        w2_scales = keep.tile([P, D], U8, name="w2_scales", align_bytes=64)
        ln_b_bank = psum_c.tile([P, 2 * D], F32, name="ln_b_bank")
        ln_g_b = keep.tile([P, D], F32, name="ln_g_b")

        banks = {}
        grouped = {}
        codes = {}
        planes = {}
        z_banks = {}
        g_grouped = {}
        g_codes = {}
        o_banks = {}
        o_t = {}
        y_banks = {}
        moments = {}
        res = {}

        def transposes(key):
            words = src[key][:].bitcast(F32)
            for b in range(2):
                if key == "w":
                    tp = psum_y.tile([P, 2, 2 * P], F32, name="y")
                else:
                    tp = psum_t.tile([P, 2, 2 * P], F32, name="tp")
                for jj in range(2):
                    for u in range(2):
                        nc.tensor.transpose(
                            tp[:, u, jj * P:(jj + 1) * P],
                            words[:, 2 * b + jj, u * P:(u + 1) * P],
                            ident[:],
                        )
                banks[(key, b)] = tp

        def copy_half(key, b, engine="scalar"):
            if b == 0:
                grouped[key] = three.tile([P, 4 * GROUP], BF16, name="grouped", align_bytes=64)
            words = grouped[key][:].bitcast(F32).rearrange("p (t u) -> p t u", u=2)
            dst = words[:, b * 2 * P:(b + 1) * 2 * P, :]
            source = banks[(key, b)][:].rearrange("p u t -> p t u")
            if engine == "vector":
                nc.vector.tensor_copy(out=dst, in_=source)
            else:
                nc.scalar.copy(out=dst, in_=source)

        def quantise(g):
            codes[g] = (four.tile([P, GROUP], U32, name="h_codes", align_bytes=64),
                        four.tile([P, GROUP], U8, name="h_scales", align_bytes=64))
            nc.vector.quantize_mx(out=codes[g][0][:].bitcast(FP8X4), scales=codes[g][1][:],
                                  in_=grouped[g][:])

        def quantise_first_weight(b):
            cols = slice(b * 2 * P, (b + 1) * 2 * P)
            nc.vector.quantize_mx(out=w1_codes[:, cols].bitcast(FP8X4), scales=w1_scales[:, cols],
                                  in_=grouped["w"][:, b * 8 * P:(b + 1) * 8 * P])

        def second_weight():
            words = w2_sb[:].bitcast(F32).rearrange("p a (q u) -> p a q u", u=2)
            tp = psum_y.tile([P, 2, D], F32, name="y")
            for a in range(2):
                for u in range(2):
                    nc.tensor.transpose(tp[:, u, a * P:(a + 1) * P], words[:, a, :, u], ident[:])
            t = keep.tile([P, 4 * D], BF16, name="w2_grouped", align_bytes=64)
            nc.vector.tensor_copy(out=t[:].bitcast(F32).rearrange("p (d u) -> p d u", u=2),
                                  in_=tp[:].rearrange("p u d -> p d u"))
            nc.vector.quantize_mx(out=w2_codes[:].bitcast(FP8X4), scales=w2_scales[:], in_=t[:])

        def constants():
            nc.tensor.matmul(out=ln_b_bank[:, 0:D], lhsT=ones[:], rhs=rows[:, D:2 * D],
                             start=True, stop=True)
            bank = psum_o.tile([P, GROUP], F32, name="o")
            nc.tensor.matmul(out=bank[:, 0:D], lhsT=sixteens[:], rhs=rows[:, 0:D],
                             start=True, stop=True)
            nc.scalar.copy(out=ln_g_b[:], in_=bank[:, 0:D])

        def first_pass(g, c):
            z = psum_z.tile([P, GROUP], F32, name="z")
            nc.tensor.matmul_mx(
                out=z[:],
                lhsT=w1_codes[:, c * P:(c + 1) * P].bitcast(FP8X4),
                lhsT_scale=w1_scales[:, c * P:(c + 1) * P],
                rhs=codes[g][0][:].bitcast(FP8X4),
                rhs_scale=codes[g][1][:],
                start=True, stop=True,
            )
            z_banks[(g, c)] = z

        def gelu(g, c):
            if c == 0:
                planes[g] = two.tile([P, TILES, GROUP], BF16, name="planes")
            nc.scalar.activation(out=planes[g][:, c, :], in_=z_banks[(g, c)][:], func=ACT.Gelu,
                                 bias=b1_c[:, c:c + 1], scale=1.0)
            ahead_g, ahead_c = (g, c + 2) if c < 2 else (g + 1, c - 2)
            if ahead_g < N_GROUPS:
                first_pass(ahead_g, ahead_c)

        def regrouped(g):
            g_grouped[g] = three.tile([P, GROUP, 4], BF16, name="g_grouped", align_bytes=64)

        def regroup_on_pool(g):
            nc.gpsimd.tensor_scalar(
                out=g_grouped[g][:, :POOL_TOKENS, :],
                in0=planes[g][:, :, :POOL_TOKENS].rearrange("p t w -> p w t"),
                scalar1=1.0, scalar2=0.0, op0=ALU.mult, op1=ALU.add)

        def regroup_on_scalar(g, hi):
            lo = POOL_TOKENS
            nc.scalar.copy(
                out=g_grouped[g][:, lo:hi, :].rearrange("p (c i) t -> p c t i", i=4),
                in_=planes[g][:, :, lo:hi].rearrange("p t (c i) -> p c t i", i=4),
            )

        def regroup(g, lo):
            nc.vector.tensor_copy(
                out=g_grouped[g][:, lo:, :].rearrange("p (c i) t -> p c t i", i=4),
                in_=planes[g][:, :, lo:].rearrange("p t (c i) -> p c t i", i=4),
            )

        def quantise_g(g):
            g_codes[g] = (two.tile([P, GROUP], U32, name="g_codes", align_bytes=64),
                          two.tile([P, GROUP], U8, name="g_scales", align_bytes=64))
            nc.vector.quantize_mx(out=g_codes[g][0][:].bitcast(FP8X4), scales=g_codes[g][1][:],
                                  in_=g_grouped[g][:].rearrange("p w j -> p (w j)"))

        def second_pass(g, a):
            if g == N_GROUPS - 1 and a == 1:
                o = psum_z.tile([P, GROUP], F32, name="z")
            else:
                o = psum_o.tile([P, GROUP], F32, name="o")
            nc.tensor.matmul_mx(
                out=o[:],
                lhsT=w2_codes[:, a * P:(a + 1) * P].bitcast(FP8X4),
                lhsT_scale=w2_scales[:, a * P:(a + 1) * P],
                rhs=g_codes[g][0][:].bitcast(FP8X4),
                rhs_scale=g_codes[g][1][:],
                start=True, stop=True,
            )
            o_banks[(g, a)] = o

        def evacuate(g, a):
            if a == 0:
                o_t[g] = two.tile([P, 2, GROUP], F32, name="o_t")
            nc.scalar.activation(out=o_t[g][:, a, :], in_=o_banks[(g, a)][:], func=ACT.Identity,
                                 bias=b2_c[:, a:a + 1], scale=1.0)

        def add_x(g):
            for b in range(2):
                y = psum_y.tile([P, 2, D], F32, name="y")
                nc.tensor.matmul(out=y[:], lhsT=ident_b[:], rhs=x_sb[g][:, 2 * b:2 * b + 2, :],
                                 start=True, stop=False)
                y_banks[(g, b)] = y

        def add_product(g, a):
            for j in range(TILES):
                b, jj = j // 2, j % 2
                nc.tensor.matmul(out=y_banks[(g, b)][:, jj, a * P:(a + 1) * P],
                                 lhsT=o_t[g][:, a, j * P:(j + 1) * P], rhs=ident[:],
                                 is_transpose=True, start=False, stop=(a == 1 and jj == 1))

        def moments_and_gain(g):
            moments[g] = (four.tile([P, TILES, 3], F32, name="moments"),
                          four.tile([P, TILES], F32, name="sum_eps"),
                          four.tile([P, TILES], F32, name="rstd"))
            res[g] = four.tile([P, TILES, D], F32, name="res")
            for b in range(2):
                nc.vector.bn_stats(out=moments[g][0][:, 2 * b:2 * b + 2, :].rearrange("p j s -> p (j s)"),
                                   in_=y_banks[(g, b)][:].rearrange("p j d -> p d j"))
            for j in range(TILES):
                nc.vector.scalar_tensor_tensor(
                    out=res[g][:, j, :], in0=y_banks[(g, j // 2)][:, j % 2, :],
                    scalar=moments[g][0][:, j, 1:2], in1=ln_g_b[:], op0=ALU.subtract, op1=ALU.mult)
                if j < 2 and g == N_GROUPS - 1:
                    add_eps(g, 2 * j, 2 * j + 2)
                    inverse_deviation(g, 2 * j, 2 * j + 2)

        def add_eps(g, lo=0, hi=TILES):
            nc.vector.tensor_scalar_add(out=moments[g][1][:, lo:hi], in0=moments[g][0][:, lo:hi, 2],
                                        scalar1=D * LN_EPS)

        def inverse_deviation(g, lo=0, hi=TILES):
            nc.gpsimd.tensor_tensor(out=moments[g][2][:, lo:hi], in0=moments[g][1][:, lo:hi],
                                    in1=minus_half[:, lo:hi], op=ALU.pow)

        def scale_and_shift(g):
            for j in range(TILES):
                nc.vector.scalar_tensor_tensor(
                    out=res[g][:, j, :], in0=res[g][:, j, :], scalar=moments[g][2][:, j:j + 1],
                    in1=ln_b_bank[:, 0:D], op0=ALU.mult, op1=ALU.add,
                )
                if g == N_GROUPS - 1:
                    nc.sync.dma_start(out=out_view[g][:, j, :], in_=res[g][:, j, :])
            if g < N_GROUPS - 1:
                nc.sync.dma_start(out=out_view[g], in_=res[g][:])

        def have(g):
            return 0 <= g < N_GROUPS

        transposes(0)
        transposes("w")
        copy_half(0, 0)
        copy_half(0, 1, "vector")
        copy_half("w", 0)
        copy_half("w", 1)
        quantise(0)
        quantise_first_weight(0)
        quantise_first_weight(1)
        second_weight()
        constants()
        first_pass(0, 0)
        first_pass(0, 1)
        transposes(1)
        copy_half(1, 0, "vector")
        copy_half(1, 1, "vector")
        quantise(1)

        for i in range(N_GROUPS + 3):
            early = i < EARLY_GROUPS
            late = i >= N_GROUPS - LATE_GROUPS
            if have(i):
                gelu(i, 0)
                gelu(i, 1)
            if i == 0:
                transposes(2)
            if have(i + 2) and not early:
                copy_half(i + 2, 0)
            if have(i - 2):
                moments_and_gain(i - 2)
            if have(i - 1):
                second_pass(i - 1, 0)
            if have(i):
                gelu(i, 2)
                gelu(i, 3)
            if have(i - 1):
                evacuate(i - 1, 0)
                second_pass(i - 1, 1)
                add_x(i - 1)
            if have(i + 2):
                copy_half(i + 2, 0 if early else 1)
            if have(i + 3) and not early:
                transposes(i + 3)
            if have(i - 1):
                add_product(i - 1, 0)
            if have(i):
                regrouped(i)
                if early:
                    regroup(i, 0)
                    quantise_g(i)
                else:
                    regroup_on_pool(i)
                    regroup_on_scalar(i, GROUP if late else POOL_TOKENS + SCALAR_TOKENS)
            if have(i - 1):
                evacuate(i - 1, 1)
                add_product(i - 1, 1)
            if early:
                copy_half(i + 2, 1)
                transposes(i + 3)
            if have(i - 3):
                scale_and_shift(i - 3)
            if have(i) and not early and not late:
                regroup(i, POOL_TOKENS + SCALAR_TOKENS)
            if have(i + 2):
                quantise(i + 2)
            if have(i) and not early:
                quantise_g(i)
            if have(i - 2) and i - 2 < N_GROUPS - 1:
                add_eps(i - 2)
                inverse_deviation(i - 2)
